import numpy as np
import ml_dtypes


def mxq(x, axis, fmt="e4m3"):
    dtype, down = {"e4m3": (ml_dtypes.float8_e4m3fn, 7), "e5m2": (ml_dtypes.float8_e5m2, 14)}[fmt]
    v = np.moveaxis(np.asarray(x, np.float32).astype(ml_dtypes.bfloat16).astype(np.float64), axis, -1)
    blocks = v.reshape(v.shape[:-1] + (-1, 32))
    amax = np.abs(blocks).max(-1, keepdims=True)
    byte = np.maximum(np.where(amax > 0, np.frexp(amax)[1] - 1 + 127, 0) - down, 1)
    scale = np.exp2(byte - 127.0)
    codes = (blocks / scale).astype(np.float32).astype(dtype).astype(np.float64)
    return np.moveaxis((codes * scale).reshape(v.shape), -1, axis)


WIDE = False


def mx_kscale(k):
    if not WIDE:
        return np.ones(k)
    levels = np.array([10, -10, 5, -5, 0])
    a = np.random.permutation(np.resize(levels, k // 512 * 4)).reshape(k // 512, 4)
    idx = np.arange(k)
    return np.exp2(a[idx // 512, idx % 128 // 32])


BF16 = ml_dtypes.bfloat16


def bf(x):
    return np.asarray(x, np.float32).astype(BF16)


def f64(x):
    return np.asarray(x).astype(np.float64)


B, Nb1, Nw1, Nb2x, Nb2y, Nw2x, Nw2y, R, C = 128, 4, 16, 4, 2, 16, 16, 128, 2
J1 = Nb1 * Nb1
K1 = C * Nw1 * Nw1
J3 = Nb2x * Nb2y
L1 = J3 * R
J2 = J3 * J1


def setup_inputs():
    s = mx_kscale(K1)
    sx = s.reshape(Nw1, Nw1, C)[:, None, :, :]
    x = np.random.standard_normal((B, Nb1, Nw1, Nb1, Nw1, C)) * sx
    return {"x": bf(x.reshape(B, Nb1 * Nw1 * Nb1 * Nw1, C)),
            "k1": bf(np.random.standard_normal((J1, K1, L1)) / np.sqrt(K1) / s[None, :, None]),
            "b1": bf(np.random.standard_normal((1, J1, L1)) * 0.3)}


def reference(x, k1, b1):
    h = f64(x).reshape(B, Nb1, Nw1, Nb1, Nw1, C).transpose(0, 1, 3, 2, 4, 5).reshape(B, J1, K1)
    hq = mxq(h, 2, "e4m3").transpose(1, 0, 2)
    y = (hq @ mxq(f64(k1), 1, "e4m3")).transpose(1, 0, 2) + f64(b1)
    y = y.reshape(B, J1, J3, R).transpose(0, 3, 1, 2)
    return y.reshape(B, J2, R)

@@ -1,0 +1,221 @@
+from contextlib import ExitStack
+
+import concourse.mybir as mybir
+from concourse.masks import make_identity
+
+BF16 = mybir.dt.bfloat16
+F32 = mybir.dt.float32
+U32 = mybir.dt.uint32
+U8 = mybir.dt.uint8
+FP8X4 = mybir.dt.float8_e4m3fn_x4
+ADD = mybir.AluOpType.add
+
+P = 128
+NJ = 16
+K1 = 512
+L1 = 1024
+NM = 8
+NR = 128
+RS = 32
+NS = NR // RS
+NCOL = NM * RS
+ND = 5
+NRAW = 7
+NGRP = 8
+KB = 1024
+
+FLOPS = 2 * P * K1 * L1 * NJ
+
+
+def on_vector(j, s):
+    return s == 0 or (s == 2 and j < NJ - ND and j % 4 != 3)
+
+
+def tile_switchnet_fstar_pa_kernel(tc, x, k1, b1, out):
+    nc = tc.nc
+    with ExitStack() as ctx:
+        keep = ctx.enter_context(tc.tile_pool(name="keep", bufs=1))
+        stage = ctx.enter_context(tc.tile_pool(name="stage", bufs=1))
+        psum = ctx.enter_context(tc.psum_pool(name="psum", bufs=8))
+
+        ident_f = keep.tile([P, P], F32)
+        b_rows = keep.tile([P, P], BF16)
+        bias = keep.tile([P, NR * P], BF16)
+        kcodes = keep.tile([P, NJ, L1], U32, align_bytes=64)
+        kscales = keep.tile([P, NJ, L1], U8, align_bytes=64)
+        xcodes = keep.tile([P, NJ * P], U32, align_bytes=64)
+        xscales = keep.tile([P, NJ * P], U8, align_bytes=64)
+
+        GRP0 = NRAW * 8 * KB
+        BIG0 = GRP0 + NGRP * 2 * KB
+
+        nc.sync.dma_start(out=b_rows[:], in_=b1.rearrange("o j (m r) -> (o j m) r", r=NR))
+        make_identity(nc, ident_f[:])
+
+        raws = {}
+
+        def load_k(j):
+            raw = stage.tile([P, 4, L1], BF16, name="raw%d" % j, offset=(j % NRAW) * 8 * KB, align_bytes=64)
+            nc.sync.dma_start(out=raw[:], in_=k1[j].rearrange("(p t) l -> p t l", t=4))
+            raws[j] = raw
+
+        b_words = b_rows[:].bitcast(F32)
+        bias_words = bias[:].bitcast(F32)
+
+        def bias_group(g):
+            pb = psum.tile([P, 4, P], F32, name="pb", tag="bank")
+            for c in range(4):
+                w = g * 4 + c
+                nc.tensor.transpose(pb[:, c, :], b_words[:, w:w + 1].to_broadcast([P, P]), ident_f[:])
+            nc.scalar.copy(out=bias_words[:, g * 512:(g + 1) * 512], in_=pb[:].rearrange("p c g -> p (c g)"))
+
+        x_rows = x.rearrange("b (a g) c -> b a (g c)", a=4)
+        x_parts = {}
+
+        def load_x(a):
+            x_sb = stage.tile([P, 2048], BF16, name="x_sb%d" % a, offset=BIG0 + a * 4 * KB, align_bytes=64)
+            nc.sync.dma_start(out=x_sb[:], in_=x_rows[:, a, :])
+            x_parts[a] = x_sb
+
+        def do_x(a):
+            xb = stage.tile([P, 2048], BF16, name="xb%d" % a, offset=BIG0 + (16 + 4 * (a % 2)) * KB, align_bytes=64)
+            nc.vector.tensor_copy(
+                out=xb[:].rearrange("p (c i w) -> p c i w", c=4, i=16),
+                in_=x_parts[a][:].rearrange("p (i c w) -> p c i w", c=4, i=16),
+            )
+            xb32 = xb[:].bitcast(F32)
+            gx = stage.tile([P, 2048], BF16, name="gx%d" % a, offset=BIG0 + (24 + 4 * (a % 2)) * KB, align_bytes=64)
+            gx32 = gx[:].bitcast(F32).rearrange("p (j b u) -> p j b u", j=4, u=2)
+            for q in range(2):
+                xt = psum.tile([P, 2, 2, P], F32, name="xt", tag="bank")
+                for jj in range(2):
+                    c = 2 * q + jj
+                    for u in range(2):
+                        nc.tensor.transpose(
+                            xt[:, jj, u, :],
+                            xb32[:, c * 256 + u:(c + 1) * 256:2],
+                            ident_f[:],
+                        )
+                nc.scalar.copy(
+                    out=gx32[:, 2 * q:2 * q + 2],
+                    in_=xt[:].rearrange("p j u b -> p j b u"),
+                )
+            nc.vector.quantize_mx(
+                out=xcodes[:, a * 512:(a + 1) * 512].bitcast(FP8X4),
+                scales=xscales[:, a * 512:(a + 1) * 512],
+                in_=gx[:],
+            )
+
+        count = [0]
+        pending = []
+
+        def quantise():
+            j, s, grouped = pending.pop(0)
+            cols = slice(s * NCOL, (s + 1) * NCOL)
+            nc.vector.quantize_mx(
+                out=kcodes[:, j, cols].bitcast(FP8X4),
+                scales=kscales[:, j, cols],
+                in_=grouped[:],
+            )
+
+        def unit(j, s, lag):
+            n = count[0]
+            count[0] = n + 1
+            grouped = stage.tile([P, 4 * NCOL], BF16, name="grp%d" % n,
+                                 offset=GRP0 + (n % NGRP) * 2 * KB, align_bytes=64)
+            src = raws[j][:].rearrange("p t (m s c i) -> p s m c t i", m=NM, s=NS, i=4)[:, s]
+            dst = grouped[:].rearrange("p (m c i t) -> p m c t i", m=NM, i=4, t=4)
+            if on_vector(j, s):
+                nc.vector.tensor_copy(out=dst, in_=src)
+            else:
+                nc.scalar.copy(out=dst, in_=src)
+            pending.append((j, s, grouped))
+            while len(pending) > lag:
+                quantise()
+
+        bias_v = bias[:].rearrange("p (w g e) -> p w e g", g=P, e=2)
+        osl_offset = [BIG0, BIG0 + 16 * KB, ((NJ - ND - 2) % NRAW) * 8 * KB, BIG0]
+
+        def do_slice(s, parts):
+            osl = stage.tile([P, RS, P], F32, name="osl%d" % s, offset=osl_offset[s], align_bytes=64)
+            osl_v = osl[:].rearrange("p (w e) g -> p w e g", e=2)
+            banks = []
+            for q in range(8):
+                ps = psum.tile([P, 512], F32, name="ps", tag="bank")
+                banks.append(ps)
+                for jj in range(2):
+                    j = 2 * q + jj
+                    nc.tensor.matmul_mx(
+                        out=ps[:, jj * NCOL:(jj + 1) * NCOL],
+                        lhsT=xcodes[:, j * P:(j + 1) * P].bitcast(FP8X4),
+                        lhsT_scale=xscales[:, j * P:(j + 1) * P],
+                        rhs=kcodes[:, j, s * NCOL:(s + 1) * NCOL].bitcast(FP8X4),
+                        rhs_scale=kscales[:, j, s * NCOL:(s + 1) * NCOL],
+                        start=True,
+                        stop=True,
+                    )
+                if parts == 1:
+                    nc.vector.tensor_tensor(
+                        out=osl_v[:, :, :, q * 16:(q + 1) * 16],
+                        in0=ps[:].rearrange("p (g w e) -> p w e g", g=16, e=2),
+                        in1=bias_v[:, s * 16:(s + 1) * 16, :, q * 16:(q + 1) * 16],
+                        op=ADD,
+                    )
+            if parts == 1:
+                nc.sync.dma_start(out=out[:, s * RS:(s + 1) * RS, :], in_=osl[:])
+            else:
+                nw = 16 // parts
+                for h in range(parts):
+                    for q in range(8):
+                        nc.vector.tensor_tensor(
+                            out=osl_v[:, h * nw:(h + 1) * nw, :, q * 16:(q + 1) * 16],
+                            in0=banks[q][:].rearrange("p (g w e) -> p w e g", g=16, e=2)[:, h * nw:(h + 1) * nw],
+                            in1=bias_v[:, s * 16 + h * nw:s * 16 + (h + 1) * nw, :, q * 16:(q + 1) * 16],
+                            op=ADD,
+                        )
+                    nr = RS // parts
+                    nc.sync.dma_start(out=out[:, s * RS + h * nr:s * RS + (h + 1) * nr, :],
+                                      in_=osl[:, h * nr:(h + 1) * nr, :])
+
+        for j in range(NRAW):
+            load_k(j)
+            if j < 4:
+                load_x(j)
+        nbias = [0]
+
+        def next_bias(limit):
+            if nbias[0] < limit:
+                bias_group(nbias[0])
+                nbias[0] += 1
+
+        next_bias(16)
+        next_bias(16)
+        for j in range(NJ):
+            unit(j, 0, 3)
+            unit(j, 1, 3)
+            if j < NJ - ND:
+                unit(j, 2, 3)
+                unit(j, 3, 3)
+                if j + NRAW < NJ:
+                    load_k(j + NRAW)
+            next_bias(8)
+            if j < 4:
+                do_x(j)
+        while pending:
+            quantise()
+        do_slice(0, 1)
+        for j in range(NJ - ND, NJ):
+            unit(j, 2, 1)
+            next_bias(16)
+        while pending:
+            quantise()
+        do_slice(1, 1)
+        for j in range(NJ - ND, NJ):
+            unit(j, 3, 1)
+            next_bias(16)
+        while pending:
+            quantise()
+        while nbias[0] < 16:
+            next_bias(16)
+        do_slice(2, 1)
+        do_slice(3, 2)

@@ -9,6 +9,7 @@ U32 = mybir.dt.uint32
 U8 = mybir.dt.uint8
 FP8X4 = mybir.dt.float8_e4m3fn_x4
 ADD = mybir.AluOpType.add
+MULT = mybir.AluOpType.mult
 
 P = 128
 NJ = 16
@@ -19,16 +20,303 @@ NR = 128
 RS = 32
 NS = NR // RS
 NCOL = NM * RS
-ND = 5
-NRAW = 7
 NGRP = 8
 KB = 1024
+RAW_SLOT = [0,8192,16384,24576,32768,40960,49152,0,8192,16384,24576,32768,40960,49152,0,8192]
+OSL_OFF = [73728,90112,16384,73728]
+GRP0 = 57344
+BIG0 = 73728
 
 FLOPS = 2 * P * K1 * L1 * NJ
 
-
-def on_vector(j, s):
-    return s == 0 or (s == 2 and j < NJ - ND and j % 4 != 3)
+ACTIONS = [
+    ("B",),
+    ("K", 0),
+    ("X", 0),
+    ("K", 1),
+    ("X", 1),
+    ("K", 2),
+    ("X", 2),
+    ("K", 3),
+    ("X", 3),
+    ("K", 4),
+    ("K", 5),
+    ("K", 6),
+    ("BT", 0),
+    ("BT", 1),
+    ("BE", 0, "S"),
+    ("BT", 2),
+    ("BE", 1, "S"),
+    ("BT", 3),
+    ("U", 0, 0, "V", 0),
+    ("U", 0, 1, "S", 1),
+    ("Q", 0, 0),
+    ("U", 0, 2, "V", 2),
+    ("U", 0, 3, "S", 3),
+    ("Q", 0, 2),
+    ("XR", 0),
+    ("K", 7),
+    ("XT", 0, 0),
+    ("XT", 0, 1),
+    ("U", 1, 0, "V", 4),
+    ("U", 1, 1, "S", 5),
+    ("Q", 0, 1),
+    ("Q", 1, 0),
+    ("XE", 0, 0, "S"),
+    ("U", 1, 2, "V", 6),
+    ("Q", 0, 3),
+    ("XE", 0, 1, "S"),
+    ("Q", 1, 2),
+    ("XR", 1),
+    ("U", 1, 3, "S", 7),
+    ("XT", 1, 0),
+    ("U", 2, 0, "V", 0),
+    ("BE", 2, "S"),
+    ("K", 8),
+    ("XT", 1, 1),
+    ("Q", 1, 1),
+    ("U", 2, 1, "S", 1),
+    ("BT", 4),
+    ("Q", 2, 0),
+    ("XQ", 0),
+    ("U", 2, 2, "V", 2),
+    ("XE", 1, 0, "S"),
+    ("Q", 1, 3),
+    ("XE", 1, 1, "S"),
+    ("Q", 2, 2),
+    ("XR", 2),
+    ("U", 2, 3, "S", 3),
+    ("U", 3, 0, "V", 4),
+    ("XT", 2, 0),
+    ("Q", 2, 1),
+    ("XT", 2, 1),
+    ("BE", 3, "S"),
+    ("K", 9),
+    ("Q", 3, 0),
+    ("XQ", 1),
+    ("U", 3, 1, "S", 5),
+    ("BT", 5),
+    ("U", 3, 2, "V", 6),
+    ("Q", 2, 3),
+    ("XE", 2, 0, "S"),
+    ("Q", 3, 2),
+    ("XR", 3),
+    ("XE", 2, 1, "S"),
+    ("U", 4, 0, "V", 0),
+    ("U", 3, 3, "S", 7),
+    ("XT", 3, 0),
+    ("Q", 3, 1),
+    ("XT", 3, 1),
+    ("Q", 4, 0),
+    ("XQ", 2),
+    ("BE", 4, "S"),
+    ("BT", 6),
+    ("K", 10),
+    ("BT", 7),
+    ("U", 4, 2, "V", 2),
+    ("U", 4, 1, "S", 1),
+    ("MM", 0, 0),
+    ("MM", 0, 1),
+    ("Q", 3, 3),
+    ("Q", 4, 2),
+    ("U", 5, 0, "V", 4),
+    ("XE", 3, 0, "S"),
+    ("Q", 4, 1),
+    ("XE", 3, 1, "S"),
+    ("Q", 5, 0),
+    ("MM", 0, 2),
+    ("U", 4, 3, "S", 3),
+    ("XQ", 3),
+    ("U", 5, 2, "V", 6),
+    ("BE", 5, "S"),
+    ("Q", 4, 3),
+    ("K", 11),
+    ("Q", 5, 2),
+    ("U", 5, 1, "S", 5),
+    ("U", 6, 0, "V", 0),
+    ("U", 5, 3, "S", 7),
+    ("Q", 5, 1),
+    ("Q", 6, 0),
+    ("U", 6, 2, "V", 2),
+    ("BE", 6, "S"),
+    ("K", 12),
+    ("Q", 5, 3),
+    ("Q", 6, 2),
+    ("U", 6, 1, "S", 1),
+    ("U", 7, 0, "V", 4),
+    ("U", 6, 3, "S", 3),
+    ("Q", 6, 1),
+    ("Q", 7, 0),
+    ("U", 7, 2, "V", 6),
+    ("MM", 0, 3),
+    ("BE", 7, "S"),
+    ("K", 13),
+    ("Q", 6, 3),
+    ("Q", 7, 2),
+    ("U", 7, 1, "S", 5),
+    ("U", 8, 0, "V", 0),
+    ("U", 7, 3, "S", 7),
+    ("Q", 7, 1),
+    ("Q", 8, 0),
+    ("U", 8, 2, "V", 2),
+    ("U", 8, 1, "S", 1),
+    ("K", 14),
+    ("Q", 7, 3),
+    ("Q", 8, 2),
+    ("U", 9, 0, "V", 4),
+    ("U", 8, 3, "S", 3),
+    ("Q", 8, 1),
+    ("Q", 9, 0),
+    ("U", 9, 2, "V", 6),
+    ("MM", 0, 4),
+    ("U", 9, 1, "S", 5),
+    ("K", 15),
+    ("Q", 8, 3),
+    ("Q", 9, 2),
+    ("U", 10, 0, "V", 0),
+    ("U", 9, 3, "S", 7),
+    ("Q", 9, 1),
+    ("Q", 10, 0),
+    ("U", 10, 2, "V", 2),
+    ("U", 10, 1, "S", 1),
+    ("Q", 9, 3),
+    ("Q", 10, 2),
+    ("U", 11, 0, "V", 4),
+    ("U", 10, 3, "S", 3),
+    ("Q", 10, 1),
+    ("Q", 11, 0),
+    ("U", 12, 0, "V", 6),
+    ("MM", 0, 5),
+    ("U", 11, 1, "S", 5),
+    ("Q", 10, 3),
+    ("Q", 12, 0),
+    ("U", 13, 0, "V", 0),
+    ("U", 12, 1, "S", 7),
+    ("Q", 11, 1),
+    ("Q", 13, 0),
+    ("U", 14, 0, "V", 2),
+    ("MM", 0, 6),
+    ("U", 13, 1, "S", 1),
+    ("Q", 12, 1),
+    ("Q", 14, 0),
+    ("U", 15, 0, "V", 4),
+    ("U", 14, 1, "S", 3),
+    ("Q", 13, 1),
+    ("Q", 15, 0),
+    ("MM", 0, 7),
+    ("U", 15, 1, "S", 5),
+    ("Q", 14, 1),
+    ("U", 11, 2, "S", 6),
+    ("Q", 15, 1),
+    ("O", 0),
+    ("E", 0, 0, 0, 16),
+    ("E", 0, 1, 0, 16),
+    ("BT", 8),
+    ("U", 12, 2, "S", 7),
+    ("E", 0, 2, 0, 16),
+    ("BT", 9),
+    ("E", 0, 3, 0, 16),
+    ("U", 13, 2, "S", 0),
+    ("BT", 10),
+    ("E", 0, 4, 0, 16),
+    ("BT", 11),
+    ("U", 14, 2, "S", 1),
+    ("E", 0, 5, 0, 16),
+    ("MM", 1, 0),
+    ("E", 0, 6, 0, 16),
+    ("MM", 1, 1),
+    ("U", 15, 2, "S", 2),
+    ("E", 0, 7, 0, 16),
+    ("MM", 1, 2),
+    ("Q", 11, 2),
+    ("MM", 1, 3),
+    ("ST", 0, 0, 32),
+    ("Q", 12, 2),
+    ("BE", 8, "S"),
+    ("Q", 13, 2),
+    ("Q", 14, 2),
+    ("BE", 9, "S"),
+    ("MM", 1, 4),
+    ("O", 1),
+    ("E", 1, 0, 0, 16),
+    ("BE", 10, "S"),
+    ("MM", 1, 5),
+    ("E", 1, 1, 0, 16),
+    ("BE", 11, "S"),
+    ("MM", 1, 6),
+    ("E", 1, 2, 0, 16),
+    ("U", 11, 3, "S", 3),
+    ("MM", 1, 7),
+    ("E", 1, 3, 0, 16),
+    ("BT", 12),
+    ("BT", 13),
+    ("E", 1, 4, 0, 16),
+    ("BT", 14),
+    ("U", 12, 3, "S", 4),
+    ("BT", 15),
+    ("E", 1, 5, 0, 16),
+    ("MM", 2, 0),
+    ("E", 1, 6, 0, 16),
+    ("U", 13, 3, "S", 5),
+    ("MM", 2, 1),
+    ("E", 1, 7, 0, 16),
+    ("MM", 2, 2),
+    ("U", 14, 3, "S", 6),
+    ("Q", 15, 2),
+    ("MM", 2, 3),
+    ("ST", 1, 0, 32),
+    ("Q", 11, 3),
+    ("Q", 12, 3),
+    ("Q", 13, 3),
+    ("U", 15, 3, "S", 7),
+    ("O", 2),
+    ("E", 2, 0, 0, 16),
+    ("E", 2, 1, 0, 16),
+    ("BE", 12, "S"),
+    ("E", 2, 2, 0, 16),
+    ("BE", 13, "S"),
+    ("MM", 2, 4),
+    ("E", 2, 3, 0, 16),
+    ("BE", 14, "S"),
+    ("MM", 2, 5),
+    ("E", 2, 4, 0, 16),
+    ("BE", 15, "S"),
+    ("MM", 2, 6),
+    ("E", 2, 5, 0, 16),
+    ("MM", 2, 7),
+    ("E", 2, 6, 0, 16),
+    ("MM", 3, 0),
+    ("MM", 3, 1),
+    ("E", 2, 7, 0, 16),
+    ("MM", 3, 2),
+    ("MM", 3, 3),
+    ("Q", 14, 3),
+    ("MM", 3, 4),
+    ("ST", 2, 0, 32),
+    ("Q", 15, 3),
+    ("MM", 3, 5),
+    ("O", 3),
+    ("E", 3, 0, 0, 8),
+    ("MM", 3, 6),
+    ("MM", 3, 7),
+    ("E", 3, 1, 0, 8),
+    ("E", 3, 2, 0, 8),
+    ("E", 3, 3, 0, 8),
+    ("E", 3, 4, 0, 8),
+    ("E", 3, 5, 0, 8),
+    ("E", 3, 6, 0, 8),
+    ("E", 3, 7, 0, 8),
+    ("E", 3, 0, 8, 8),
+    ("ST", 3, 0, 16),
+    ("E", 3, 1, 8, 8),
+    ("E", 3, 2, 8, 8),
+    ("E", 3, 3, 8, 8),
+    ("E", 3, 4, 8, 8),
+    ("E", 3, 5, 8, 8),
+    ("E", 3, 6, 8, 8),
+    ("E", 3, 7, 8, 8),
+    ("ST", 3, 16, 16),
+]
 
 
 def tile_switchnet_fstar_pa_kernel(tc, x, k1, b1, out):
@@ -37,6 +325,7 @@ def tile_switchnet_fstar_pa_kernel(tc, x, k1, b1, out):
         keep = ctx.enter_context(tc.tile_pool(name="keep", bufs=1))
         stage = ctx.enter_context(tc.tile_pool(name="stage", bufs=1))
         psum = ctx.enter_context(tc.psum_pool(name="psum", bufs=8))
+        ctx.enter_context(tc.manual_schedule())
 
         ident_f = keep.tile([P, P], F32)
         b_rows = keep.tile([P, P], BF16)
@@ -46,103 +335,109 @@ def tile_switchnet_fstar_pa_kernel(tc, x, k1, b1, out):
         xcodes = keep.tile([P, NJ * P], U32, align_bytes=64)
         xscales = keep.tile([P, NJ * P], U8, align_bytes=64)
 
-        GRP0 = NRAW * 8 * KB
-        BIG0 = GRP0 + NGRP * 2 * KB
-
-        nc.sync.dma_start(out=b_rows[:], in_=b1.rearrange("o j (m r) -> (o j m) r", r=NR))
-        make_identity(nc, ident_f[:])
-
-        raws = {}
-
-        def load_k(j):
-            raw = stage.tile([P, 4, L1], BF16, name="raw%d" % j, offset=(j % NRAW) * 8 * KB, align_bytes=64)
-            nc.sync.dma_start(out=raw[:], in_=k1[j].rearrange("(p t) l -> p t l", t=4))
-            raws[j] = raw
-
         b_words = b_rows[:].bitcast(F32)
         bias_words = bias[:].bitcast(F32)
-
-        def bias_group(g):
-            pb = psum.tile([P, 4, P], F32, name="pb", tag="bank")
-            for c in range(4):
-                w = g * 4 + c
-                nc.tensor.transpose(pb[:, c, :], b_words[:, w:w + 1].to_broadcast([P, P]), ident_f[:])
-            nc.scalar.copy(out=bias_words[:, g * 512:(g + 1) * 512], in_=pb[:].rearrange("p c g -> p (c g)"))
-
+        bias_v = bias[:].rearrange("p (w g e) -> p w e g", g=P, e=2)
         x_rows = x.rearrange("b (a g) c -> b a (g c)", a=4)
+
+        raws = {}
         x_parts = {}
+        xbs = {}
+        gxs = {}
+        banks = {}
+        osls = {}
+        pending = {}
 
-        def load_x(a):
-            x_sb = stage.tile([P, 2048], BF16, name="x_sb%d" % a, offset=BIG0 + a * 4 * KB, align_bytes=64)
-            nc.sync.dma_start(out=x_sb[:], in_=x_rows[:, a, :])
-            x_parts[a] = x_sb
-
-        def do_x(a):
-            xb = stage.tile([P, 2048], BF16, name="xb%d" % a, offset=BIG0 + (16 + 4 * (a % 2)) * KB, align_bytes=64)
-            nc.vector.tensor_copy(
-                out=xb[:].rearrange("p (c i w) -> p c i w", c=4, i=16),
-                in_=x_parts[a][:].rearrange("p (i c w) -> p c i w", c=4, i=16),
-            )
-            xb32 = xb[:].bitcast(F32)
-            gx = stage.tile([P, 2048], BF16, name="gx%d" % a, offset=BIG0 + (24 + 4 * (a % 2)) * KB, align_bytes=64)
-            gx32 = gx[:].bitcast(F32).rearrange("p (j b u) -> p j b u", j=4, u=2)
-            for q in range(2):
-                xt = psum.tile([P, 2, 2, P], F32, name="xt", tag="bank")
-                for jj in range(2):
-                    c = 2 * q + jj
-                    for u in range(2):
-                        nc.tensor.transpose(
-                            xt[:, jj, u, :],
-                            xb32[:, c * 256 + u:(c + 1) * 256:2],
-                            ident_f[:],
-                        )
-                nc.scalar.copy(
-                    out=gx32[:, 2 * q:2 * q + 2],
-                    in_=xt[:].rearrange("p j u b -> p j b u"),
-                )
-            nc.vector.quantize_mx(
-                out=xcodes[:, a * 512:(a + 1) * 512].bitcast(FP8X4),
-                scales=xscales[:, a * 512:(a + 1) * 512],
-                in_=gx[:],
-            )
-
-        count = [0]
-        pending = []
-
-        def quantise():
-            j, s, grouped = pending.pop(0)
-            cols = slice(s * NCOL, (s + 1) * NCOL)
-            nc.vector.quantize_mx(
-                out=kcodes[:, j, cols].bitcast(FP8X4),
-                scales=kscales[:, j, cols],
-                in_=grouped[:],
-            )
-
-        def unit(j, s, lag):
-            n = count[0]
-            count[0] = n + 1
-            grouped = stage.tile([P, 4 * NCOL], BF16, name="grp%d" % n,
-                                 offset=GRP0 + (n % NGRP) * 2 * KB, align_bytes=64)
-            src = raws[j][:].rearrange("p t (m s c i) -> p s m c t i", m=NM, s=NS, i=4)[:, s]
-            dst = grouped[:].rearrange("p (m c i t) -> p m c t i", m=NM, i=4, t=4)
-            if on_vector(j, s):
+        def engine_copy(eng, dst, src):
+            if eng == "V":
                 nc.vector.tensor_copy(out=dst, in_=src)
             else:
                 nc.scalar.copy(out=dst, in_=src)
-            pending.append((j, s, grouped))
-            while len(pending) > lag:
-                quantise()
 
-        bias_v = bias[:].rearrange("p (w g e) -> p w e g", g=P, e=2)
-        osl_offset = [BIG0, BIG0 + 16 * KB, ((NJ - ND - 2) % NRAW) * 8 * KB, BIG0]
-
-        def do_slice(s, parts):
-            osl = stage.tile([P, RS, P], F32, name="osl%d" % s, offset=osl_offset[s], align_bytes=64)
-            osl_v = osl[:].rearrange("p (w e) g -> p w e g", e=2)
-            banks = []
-            for q in range(8):
+        for a in ACTIONS:
+            k = a[0]
+            if k == "B":
+                nc.sync.dma_start(out=b_rows[:], in_=b1.rearrange("o j (m r) -> (o j m) r", r=NR))
+                make_identity(nc, ident_f[:])
+            elif k == "K":
+                j = a[1]
+                raw = stage.tile([P, 4, L1], BF16, name="raw%d" % j, offset=RAW_SLOT[j], align_bytes=64)
+                nc.sync.dma_start(out=raw[:], in_=k1[j].rearrange("(p t) l -> p t l", t=4))
+                raws[j] = raw
+            elif k == "X":
+                q = a[1]
+                x_sb = stage.tile([P, 2048], BF16, name="x_sb%d" % q, offset=BIG0 + q * 4 * KB, align_bytes=64)
+                nc.sync.dma_start(out=x_sb[:], in_=x_rows[:, q, :])
+                x_parts[q] = x_sb
+            elif k == "BT":
+                g = a[1]
+                pb = psum.tile([P, 4, P], F32, name="pb", tag="bank")
+                for c in range(4):
+                    w = g * 4 + c
+                    nc.tensor.transpose(pb[:, c, :], b_words[:, w:w + 1].to_broadcast([P, P]), ident_f[:])
+                banks[("b", g)] = pb
+            elif k == "BE":
+                g = a[1]
+                engine_copy(a[2], bias_words[:, g * 512:(g + 1) * 512],
+                            banks[("b", g)][:].rearrange("p c g -> p (c g)"))
+            elif k == "XR":
+                q = a[1]
+                xb = stage.tile([P, 2048], BF16, name="xb%d" % q, offset=BIG0 + (16 + 4 * (q % 2)) * KB, align_bytes=64)
+                nc.vector.tensor_copy(
+                    out=xb[:].rearrange("p (c i w) -> p c i w", c=4, i=16),
+                    in_=x_parts[q][:].rearrange("p (i c w) -> p c i w", c=4, i=16),
+                )
+                xbs[q] = xb
+                gxs[q] = stage.tile([P, 2048], BF16, name="gx%d" % q, offset=BIG0 + (24 + 4 * (q % 2)) * KB, align_bytes=64)
+            elif k == "XT":
+                q, h = a[1], a[2]
+                xb32 = xbs[q][:].bitcast(F32)
+                xt = psum.tile([P, 2, 2, P], F32, name="xt", tag="bank")
+                for jj in range(2):
+                    c = 2 * h + jj
+                    for u in range(2):
+                        nc.tensor.transpose(xt[:, jj, u, :], xb32[:, c * 256 + u:(c + 1) * 256:2], ident_f[:])
+                banks[("x", q, h)] = xt
+            elif k == "XE":
+                q, h = a[1], a[2]
+                gx32 = gxs[q][:].bitcast(F32).rearrange("p (j b u) -> p j b u", j=4, u=2)
+                engine_copy(a[3], gx32[:, 2 * h:2 * h + 2], banks[("x", q, h)][:].rearrange("p j u b -> p j b u"))
+            elif k == "XQ":
+                q = a[1]
+                nc.vector.quantize_mx(
+                    out=xcodes[:, q * 512:(q + 1) * 512].bitcast(FP8X4),
+                    scales=xscales[:, q * 512:(q + 1) * 512],
+                    in_=gxs[q][:],
+                )
+            elif k == "U":
+                j, s, eng = a[1], a[2], a[3]
+                grouped = stage.tile([P, 4 * NCOL], BF16, name="grp%d_%d" % (j, s),
+                                     offset=GRP0 + a[4] * 2 * KB, align_bytes=64)
+                if eng == "G":
+                    nc.gpsimd.tensor_scalar(
+                        out=grouped[:].rearrange("p (m r t) -> p m r t", m=NM, t=4),
+                        in0=raws[j][:].rearrange("p t (m s r) -> p s m r t", m=NM, s=NS)[:, s],
+                        scalar1=1.0, scalar2=0.0, op0=MULT, op1=ADD,
+                    )
+                else:
+                    engine_copy(
+                        eng,
+                        grouped[:].rearrange("p (m c i t) -> p m c t i", m=NM, i=4, t=4),
+                        raws[j][:].rearrange("p t (m s c i) -> p s m c t i", m=NM, s=NS, i=4)[:, s],
+                    )
+                pending[(j, s)] = grouped
+            elif k == "Q":
+                j, s = a[1], a[2]
+                grouped = pending[(j, s)]
+                cols = slice(s * NCOL, (s + 1) * NCOL)
+                nc.vector.quantize_mx(
+                    out=kcodes[:, j, cols].bitcast(FP8X4),
+                    scales=kscales[:, j, cols],
+                    in_=grouped[:],
+                )
+            elif k == "MM":
+                s, q = a[1], a[2]
                 ps = psum.tile([P, 512], F32, name="ps", tag="bank")
-                banks.append(ps)
                 for jj in range(2):
                     j = 2 * q + jj
                     nc.tensor.matmul_mx(
@@ -154,68 +449,34 @@ def tile_switchnet_fstar_pa_kernel(tc, x, k1, b1, out):
                         start=True,
                         stop=True,
                     )
-                if parts == 1:
-                    nc.vector.tensor_tensor(
-                        out=osl_v[:, :, :, q * 16:(q + 1) * 16],
-                        in0=ps[:].rearrange("p (g w e) -> p w e g", g=16, e=2),
-                        in1=bias_v[:, s * 16:(s + 1) * 16, :, q * 16:(q + 1) * 16],
-                        op=ADD,
-                    )
-            if parts == 1:
-                nc.sync.dma_start(out=out[:, s * RS:(s + 1) * RS, :], in_=osl[:])
-            else:
-                nw = 16 // parts
-                for h in range(parts):
-                    for q in range(8):
-                        nc.vector.tensor_tensor(
-                            out=osl_v[:, h * nw:(h + 1) * nw, :, q * 16:(q + 1) * 16],
-                            in0=banks[q][:].rearrange("p (g w e) -> p w e g", g=16, e=2)[:, h * nw:(h + 1) * nw],
-                            in1=bias_v[:, s * 16 + h * nw:s * 16 + (h + 1) * nw, :, q * 16:(q + 1) * 16],
-                            op=ADD,
-                        )
-                    nr = RS // parts
-                    nc.sync.dma_start(out=out[:, s * RS + h * nr:s * RS + (h + 1) * nr, :],
-                                      in_=osl[:, h * nr:(h + 1) * nr, :])
-
-        for j in range(NRAW):
-            load_k(j)
-            if j < 4:
-                load_x(j)
-        nbias = [0]
-
-        def next_bias(limit):
-            if nbias[0] < limit:
-                bias_group(nbias[0])
-                nbias[0] += 1
-
-        next_bias(16)
-        next_bias(16)
-        for j in range(NJ):
-            unit(j, 0, 3)
-            unit(j, 1, 3)
-            if j < NJ - ND:
-                unit(j, 2, 3)
-                unit(j, 3, 3)
-                if j + NRAW < NJ:
-                    load_k(j + NRAW)
-            next_bias(8)
-            if j < 4:
-                do_x(j)
-        while pending:
-            quantise()
-        do_slice(0, 1)
-        for j in range(NJ - ND, NJ):
-            unit(j, 2, 1)
-            next_bias(16)
-        while pending:
-            quantise()
-        do_slice(1, 1)
-        for j in range(NJ - ND, NJ):
-            unit(j, 3, 1)
-            next_bias(16)
-        while pending:
-            quantise()
-        while nbias[0] < 16:
-            next_bias(16)
-        do_slice(2, 1)
-        do_slice(3, 2)
+                banks[("m", s, q)] = ps
+            elif k == "O":
+                s = a[1]
+                osls[s] = stage.tile([P, RS, P], F32, name="osl%d" % s, offset=OSL_OFF[s], align_bytes=64)
+            elif k == "E":
+                s, q, w0, nw = a[1], a[2], a[3], a[4]
+                osl_v = osls[s][:].rearrange("p (w e) g -> p w e g", e=2)
+                nc.vector.tensor_tensor(
+                    out=osl_v[:, w0:w0 + nw, :, q * 16:(q + 1) * 16],
+                    in0=banks[("m", s, q)][:].rearrange("p (g w e) -> p w e g", g=16, e=2)[:, w0:w0 + nw],
+                    in1=bias_v[:, s * 16 + w0:s * 16 + w0 + nw, :, q * 16:(q + 1) * 16],
+                    op=ADD,
+                )
+            elif k == "ES":
+                s, q = a[1], a[2]
+                nc.scalar.copy(
+                    out=osls[s][:, :, q * 16:(q + 1) * 16],
+                    in_=banks[("m", s, q)][:].rearrange("p (g r) -> p r g", g=16),
+                )
+            elif k == "EG":
+                s, q = a[1], a[2]
+                osl_v = osls[s][:].rearrange("p (w e) g -> p w e g", e=2)
+                nc.gpsimd.tensor_tensor(
+                    out=osl_v[:, :, :, q * 16:(q + 1) * 16],
+                    in0=osl_v[:, :, :, q * 16:(q + 1) * 16],
+                    in1=bias_v[:, s * 16:(s + 1) * 16, :, q * 16:(q + 1) * 16],
+                    op=ADD,
+                )
+            elif k == "ST":
+                s, r0, nr = a[1], a[2], a[3]
+                nc.sync.dma_start(out=out[:, s * RS + r0:s * RS + r0 + nr, :], in_=osls[s][:, r0:r0 + nr, :])

@@ -9,314 +9,50 @@ U32 = mybir.dt.uint32
 U8 = mybir.dt.uint8
 FP8X4 = mybir.dt.float8_e4m3fn_x4
 ADD = mybir.AluOpType.add
-MULT = mybir.AluOpType.mult
 
 P = 128
-NJ = 16
-K1 = 512
-L1 = 1024
-NM = 8
-NR = 128
-RS = 32
-NS = NR // RS
-NCOL = NM * RS
-NGRP = 8
+PACK = 4
+BLOCKS = 16
+K_BLOCK = P * PACK
+COLS = 1024
+M_BLOCKS = 8
+R = 128
+SLICE_R = 32
+SLICES = R // SLICE_R
+PASS_COLS = M_BLOCKS * SLICE_R
+JM = BLOCKS * M_BLOCKS
+BANK_F32 = 512
+PSUM_BANKS = 8
+BANK_BLOCKS = BANK_F32 // PASS_COLS
+X_QUARTERS = 4
+BIAS_GROUPS = 16
+
+FIRST_LATE = 11
+VECTOR_LAG = 1
+SCALAR_LAG = 4
+EARLY_BIAS_GROUPS = 8
+BIAS_AHEAD = 4
+
 KB = 1024
-RAW_SLOT = [0,8192,16384,24576,32768,40960,49152,0,8192,16384,24576,32768,40960,49152,0,8192]
-OSL_OFF = [73728,90112,16384,73728]
-GRP0 = 57344
-BIG0 = 73728
-
-FLOPS = 2 * P * K1 * L1 * NJ
-
-ACTIONS = [
-    ("B",),
-    ("K", 0),
-    ("X", 0),
-    ("K", 1),
-    ("X", 1),
-    ("K", 2),
-    ("X", 2),
-    ("K", 3),
-    ("X", 3),
-    ("K", 4),
-    ("K", 5),
-    ("K", 6),
-    ("BT", 0),
-    ("BT", 1),
-    ("BE", 0, "S"),
-    ("BT", 2),
-    ("BE", 1, "S"),
-    ("BT", 3),
-    ("U", 0, 0, "V", 0),
-    ("U", 0, 1, "S", 1),
-    ("Q", 0, 0),
-    ("U", 0, 2, "V", 2),
-    ("U", 0, 3, "S", 3),
-    ("Q", 0, 2),
-    ("XR", 0),
-    ("K", 7),
-    ("XT", 0, 0),
-    ("XT", 0, 1),
-    ("U", 1, 0, "V", 4),
-    ("U", 1, 1, "S", 5),
-    ("Q", 0, 1),
-    ("Q", 1, 0),
-    ("XE", 0, 0, "S"),
-    ("U", 1, 2, "V", 6),
-    ("Q", 0, 3),
-    ("XE", 0, 1, "S"),
-    ("Q", 1, 2),
-    ("XR", 1),
-    ("U", 1, 3, "S", 7),
-    ("XT", 1, 0),
-    ("U", 2, 0, "V", 0),
-    ("BE", 2, "S"),
-    ("K", 8),
-    ("XT", 1, 1),
-    ("Q", 1, 1),
-    ("U", 2, 1, "S", 1),
-    ("BT", 4),
-    ("Q", 2, 0),
-    ("XQ", 0),
-    ("U", 2, 2, "V", 2),
-    ("XE", 1, 0, "S"),
-    ("Q", 1, 3),
-    ("XE", 1, 1, "S"),
-    ("Q", 2, 2),
-    ("XR", 2),
-    ("U", 2, 3, "S", 3),
-    ("U", 3, 0, "V", 4),
-    ("XT", 2, 0),
-    ("Q", 2, 1),
-    ("XT", 2, 1),
-    ("BE", 3, "S"),
-    ("K", 9),
-    ("Q", 3, 0),
-    ("XQ", 1),
-    ("U", 3, 1, "S", 5),
-    ("BT", 5),
-    ("U", 3, 2, "V", 6),
-    ("Q", 2, 3),
-    ("XE", 2, 0, "S"),
-    ("Q", 3, 2),
-    ("XR", 3),
-    ("XE", 2, 1, "S"),
-    ("U", 4, 0, "V", 0),
-    ("U", 3, 3, "S", 7),
-    ("XT", 3, 0),
-    ("Q", 3, 1),
-    ("XT", 3, 1),
-    ("Q", 4, 0),
-    ("XQ", 2),
-    ("BE", 4, "S"),
-    ("BT", 6),
-    ("K", 10),
-    ("BT", 7),
-    ("U", 4, 2, "V", 2),
-    ("U", 4, 1, "S", 1),
-    ("MM", 0, 0),
-    ("MM", 0, 1),
-    ("Q", 3, 3),
-    ("Q", 4, 2),
-    ("U", 5, 0, "V", 4),
-    ("XE", 3, 0, "S"),
-    ("Q", 4, 1),
-    ("XE", 3, 1, "S"),
-    ("Q", 5, 0),
-    ("MM", 0, 2),
-    ("U", 4, 3, "S", 3),
-    ("XQ", 3),
-    ("U", 5, 2, "V", 6),
-    ("BE", 5, "S"),
-    ("Q", 4, 3),
-    ("K", 11),
-    ("Q", 5, 2),
-    ("U", 5, 1, "S", 5),
-    ("U", 6, 0, "V", 0),
-    ("U", 5, 3, "S", 7),
-    ("Q", 5, 1),
-    ("Q", 6, 0),
-    ("U", 6, 2, "V", 2),
-    ("BE", 6, "S"),
-    ("K", 12),
-    ("Q", 5, 3),
-    ("Q", 6, 2),
-    ("U", 6, 1, "S", 1),
-    ("U", 7, 0, "V", 4),
-    ("U", 6, 3, "S", 3),
-    ("Q", 6, 1),
-    ("Q", 7, 0),
-    ("U", 7, 2, "V", 6),
-    ("MM", 0, 3),
-    ("BE", 7, "S"),
-    ("K", 13),
-    ("Q", 6, 3),
-    ("Q", 7, 2),
-    ("U", 7, 1, "S", 5),
-    ("U", 8, 0, "V", 0),
-    ("U", 7, 3, "S", 7),
-    ("Q", 7, 1),
-    ("Q", 8, 0),
-    ("U", 8, 2, "V", 2),
-    ("U", 8, 1, "S", 1),
-    ("K", 14),
-    ("Q", 7, 3),
-    ("Q", 8, 2),
-    ("U", 9, 0, "V", 4),
-    ("U", 8, 3, "S", 3),
-    ("Q", 8, 1),
-    ("Q", 9, 0),
-    ("U", 9, 2, "V", 6),
-    ("MM", 0, 4),
-    ("U", 9, 1, "S", 5),
-    ("K", 15),
-    ("Q", 8, 3),
-    ("Q", 9, 2),
-    ("U", 10, 0, "V", 0),
-    ("U", 9, 3, "S", 7),
-    ("Q", 9, 1),
-    ("Q", 10, 0),
-    ("U", 10, 2, "V", 2),
-    ("U", 10, 1, "S", 1),
-    ("Q", 9, 3),
-    ("Q", 10, 2),
-    ("U", 11, 0, "V", 4),
-    ("U", 10, 3, "S", 3),
-    ("Q", 10, 1),
-    ("Q", 11, 0),
-    ("U", 12, 0, "V", 6),
-    ("MM", 0, 5),
-    ("U", 11, 1, "S", 5),
-    ("Q", 10, 3),
-    ("Q", 12, 0),
-    ("U", 13, 0, "V", 0),
-    ("U", 12, 1, "S", 7),
-    ("Q", 11, 1),
-    ("Q", 13, 0),
-    ("U", 14, 0, "V", 2),
-    ("MM", 0, 6),
-    ("U", 13, 1, "S", 1),
-    ("Q", 12, 1),
-    ("Q", 14, 0),
-    ("U", 15, 0, "V", 4),
-    ("U", 14, 1, "S", 3),
-    ("Q", 13, 1),
-    ("Q", 15, 0),
-    ("MM", 0, 7),
-    ("U", 15, 1, "S", 5),
-    ("Q", 14, 1),
-    ("U", 11, 2, "S", 6),
-    ("Q", 15, 1),
-    ("O", 0),
-    ("E", 0, 0, 0, 16),
-    ("E", 0, 1, 0, 16),
-    ("BT", 8),
-    ("U", 12, 2, "S", 7),
-    ("E", 0, 2, 0, 16),
-    ("BT", 9),
-    ("E", 0, 3, 0, 16),
-    ("U", 13, 2, "S", 0),
-    ("BT", 10),
-    ("E", 0, 4, 0, 16),
-    ("BT", 11),
-    ("U", 14, 2, "S", 1),
-    ("E", 0, 5, 0, 16),
-    ("MM", 1, 0),
-    ("E", 0, 6, 0, 16),
-    ("MM", 1, 1),
-    ("U", 15, 2, "S", 2),
-    ("E", 0, 7, 0, 16),
-    ("MM", 1, 2),
-    ("Q", 11, 2),
-    ("MM", 1, 3),
-    ("ST", 0, 0, 32),
-    ("Q", 12, 2),
-    ("BE", 8, "S"),
-    ("Q", 13, 2),
-    ("Q", 14, 2),
-    ("BE", 9, "S"),
-    ("MM", 1, 4),
-    ("O", 1),
-    ("E", 1, 0, 0, 16),
-    ("BE", 10, "S"),
-    ("MM", 1, 5),
-    ("E", 1, 1, 0, 16),
-    ("BE", 11, "S"),
-    ("MM", 1, 6),
-    ("E", 1, 2, 0, 16),
-    ("U", 11, 3, "S", 3),
-    ("MM", 1, 7),
-    ("E", 1, 3, 0, 16),
-    ("BT", 12),
-    ("BT", 13),
-    ("E", 1, 4, 0, 16),
-    ("BT", 14),
-    ("U", 12, 3, "S", 4),
-    ("BT", 15),
-    ("E", 1, 5, 0, 16),
-    ("MM", 2, 0),
-    ("E", 1, 6, 0, 16),
-    ("U", 13, 3, "S", 5),
-    ("MM", 2, 1),
-    ("E", 1, 7, 0, 16),
-    ("MM", 2, 2),
-    ("U", 14, 3, "S", 6),
-    ("Q", 15, 2),
-    ("MM", 2, 3),
-    ("ST", 1, 0, 32),
-    ("Q", 11, 3),
-    ("Q", 12, 3),
-    ("Q", 13, 3),
-    ("U", 15, 3, "S", 7),
-    ("O", 2),
-    ("E", 2, 0, 0, 16),
-    ("E", 2, 1, 0, 16),
-    ("BE", 12, "S"),
-    ("E", 2, 2, 0, 16),
-    ("BE", 13, "S"),
-    ("MM", 2, 4),
-    ("E", 2, 3, 0, 16),
-    ("BE", 14, "S"),
-    ("MM", 2, 5),
-    ("E", 2, 4, 0, 16),
-    ("BE", 15, "S"),
-    ("MM", 2, 6),
-    ("E", 2, 5, 0, 16),
-    ("MM", 2, 7),
-    ("E", 2, 6, 0, 16),
-    ("MM", 3, 0),
-    ("MM", 3, 1),
-    ("E", 2, 7, 0, 16),
-    ("MM", 3, 2),
-    ("MM", 3, 3),
-    ("Q", 14, 3),
-    ("MM", 3, 4),
-    ("ST", 2, 0, 32),
-    ("Q", 15, 3),
-    ("MM", 3, 5),
-    ("O", 3),
-    ("E", 3, 0, 0, 8),
-    ("MM", 3, 6),
-    ("MM", 3, 7),
-    ("E", 3, 1, 0, 8),
-    ("E", 3, 2, 0, 8),
-    ("E", 3, 3, 0, 8),
-    ("E", 3, 4, 0, 8),
-    ("E", 3, 5, 0, 8),
-    ("E", 3, 6, 0, 8),
-    ("E", 3, 7, 0, 8),
-    ("E", 3, 0, 8, 8),
-    ("ST", 3, 0, 16),
-    ("E", 3, 1, 8, 8),
-    ("E", 3, 2, 8, 8),
-    ("E", 3, 3, 8, 8),
-    ("E", 3, 4, 8, 8),
-    ("E", 3, 5, 8, 8),
-    ("E", 3, 6, 8, 8),
-    ("E", 3, 7, 8, 8),
-    ("ST", 3, 16, 16),
+RAW_SLOTS = 7
+RAW_BYTES = 8 * KB
+UNIT_SLOTS = 8
+UNIT_BYTES = 2 * KB
+UNIT_BASE = RAW_SLOTS * RAW_BYTES
+WIDE_BASE = UNIT_BASE + UNIT_SLOTS * UNIT_BYTES
+SLICE_BYTES = SLICE_R * JM * 4
+SLICE_BASE = [
+    WIDE_BASE,
+    WIDE_BASE + SLICE_BYTES,
+    ((FIRST_LATE - 2) % RAW_SLOTS) * RAW_BYTES,
+    WIDE_BASE,
 ]
+
+FLOPS = 2 * P * K_BLOCK * COLS * BLOCKS
+
+
+def on_vector(s):
+    return s % 2 == 0
 
 
 def tile_switchnet_fstar_pa_kernel(tc, x, k1, b1, out):
@@ -324,159 +60,213 @@ def tile_switchnet_fstar_pa_kernel(tc, x, k1, b1, out):
     with ExitStack() as ctx:
         keep = ctx.enter_context(tc.tile_pool(name="keep", bufs=1))
         stage = ctx.enter_context(tc.tile_pool(name="stage", bufs=1))
-        psum = ctx.enter_context(tc.psum_pool(name="psum", bufs=8))
+        psum = ctx.enter_context(tc.psum_pool(name="psum", bufs=PSUM_BANKS))
         ctx.enter_context(tc.manual_schedule())
 
-        ident_f = keep.tile([P, P], F32)
-        b_rows = keep.tile([P, P], BF16)
-        bias = keep.tile([P, NR * P], BF16)
-        kcodes = keep.tile([P, NJ, L1], U32, align_bytes=64)
-        kscales = keep.tile([P, NJ, L1], U8, align_bytes=64)
-        xcodes = keep.tile([P, NJ * P], U32, align_bytes=64)
-        xscales = keep.tile([P, NJ * P], U8, align_bytes=64)
+        identity = keep.tile([P, P], F32)
+        bias_rows = keep.tile([P, R], BF16)
+        bias = keep.tile([P, R * JM], BF16)
+        k_codes = keep.tile([P, BLOCKS, COLS], U32, align_bytes=64)
+        k_scales = keep.tile([P, BLOCKS, COLS], U8, align_bytes=64)
+        x_codes = keep.tile([P, BLOCKS * P], U32, align_bytes=64)
+        x_scales = keep.tile([P, BLOCKS * P], U8, align_bytes=64)
 
-        b_words = b_rows[:].bitcast(F32)
+        bias_row_words = bias_rows[:].bitcast(F32)
         bias_words = bias[:].bitcast(F32)
-        bias_v = bias[:].rearrange("p (w g e) -> p w e g", g=P, e=2)
-        x_rows = x.rearrange("b (a g) c -> b a (g c)", a=4)
+        bias_by_r = bias[:].rearrange("p (w g e) -> p w e g", g=JM, e=2)
+        x_quarters = x.rearrange("b (a g) c -> b a (g c)", a=X_QUARTERS)
 
-        raws = {}
-        x_parts = {}
-        xbs = {}
-        gxs = {}
+        raw = {}
+        grouped = {}
+        x_loaded = {}
+        x_sorted = {}
+        x_grouped = {}
         banks = {}
-        osls = {}
-        pending = {}
+        slices = {}
 
-        def engine_copy(eng, dst, src):
-            if eng == "V":
+        def bank(key, shape):
+            banks[key] = psum.tile(shape, F32, name="bank", tag="bank")
+            return banks[key]
+
+        def load_weights(j):
+            raw[j] = stage.tile([P, PACK, COLS], BF16, name="raw%d" % j,
+                                offset=(j % RAW_SLOTS) * RAW_BYTES, align_bytes=64)
+            nc.sync.dma_start(out=raw[j][:], in_=k1[j].rearrange("(p t) l -> p t l", t=PACK))
+
+        def load_x(a):
+            x_loaded[a] = stage.tile([P, 2048], BF16, name="x_loaded%d" % a,
+                                     offset=WIDE_BASE + a * 4 * KB, align_bytes=64)
+            nc.sync.dma_start(out=x_loaded[a][:], in_=x_quarters[:, a, :])
+
+        def spread_bias(g):
+            fanned = bank(("bias", g), [P, 4, JM])
+            for c in range(4):
+                w = 4 * g + c
+                nc.tensor.transpose(fanned[:, c, :], bias_row_words[:, w:w + 1].to_broadcast([P, P]), identity[:])
+
+        def copy_bias(g):
+            nc.scalar.copy(out=bias_words[:, g * BANK_F32:(g + 1) * BANK_F32],
+                           in_=banks[("bias", g)][:].rearrange("p c g -> p (c g)"))
+
+        def sort_x(a):
+            x_sorted[a] = stage.tile([P, 2048], BF16, name="x_sorted%d" % a,
+                                     offset=WIDE_BASE + (16 + 4 * (a % 2)) * KB, align_bytes=64)
+            nc.vector.tensor_copy(
+                out=x_sorted[a][:].rearrange("p (c i w) -> p c i w", c=4, i=16),
+                in_=x_loaded[a][:].rearrange("p (i c w) -> p c i w", c=4, i=16),
+            )
+            x_grouped[a] = stage.tile([P, 2048], BF16, name="x_grouped%d" % a,
+                                      offset=WIDE_BASE + (24 + 4 * (a % 2)) * KB, align_bytes=64)
+
+        def transpose_x(a):
+            words = x_sorted[a][:].bitcast(F32)
+            for h in range(2):
+                turned = bank(("x", a, h), [P, 2, 2, P])
+                for c in range(2):
+                    first = (2 * h + c) * (K_BLOCK // 2)
+                    for u in range(2):
+                        nc.tensor.transpose(turned[:, c, u, :],
+                                            words[:, first + u:first + K_BLOCK // 2:2], identity[:])
+
+        def copy_x(a):
+            words = x_grouped[a][:].bitcast(F32).rearrange("p (j b u) -> p j b u", j=4, u=2)
+            for h in range(2):
+                nc.scalar.copy(out=words[:, 2 * h:2 * h + 2],
+                               in_=banks[("x", a, h)][:].rearrange("p j u b -> p j b u"))
+
+        def quantise_x(a):
+            cols = slice(a * 4 * P, (a + 1) * 4 * P)
+            nc.vector.quantize_mx(out=x_codes[:, cols].bitcast(FP8X4), scales=x_scales[:, cols],
+                                  in_=x_grouped[a][:])
+
+        def regroup(n, j, s, vector):
+            grouped[(j, s)] = stage.tile([P, PACK * PASS_COLS], BF16, name="unit%d_%d" % (j, s),
+                                         offset=UNIT_BASE + (n % UNIT_SLOTS) * UNIT_BYTES, align_bytes=64)
+            dst = grouped[(j, s)][:].rearrange("p (m c i t) -> p m c t i", m=M_BLOCKS, i=4, t=PACK)
+            src = raw[j][:].rearrange("p t (m s c i) -> p s m c t i", m=M_BLOCKS, s=SLICES, i=4)[:, s]
+            if vector:
                 nc.vector.tensor_copy(out=dst, in_=src)
             else:
                 nc.scalar.copy(out=dst, in_=src)
 
-        for a in ACTIONS:
-            k = a[0]
-            if k == "B":
-                nc.sync.dma_start(out=b_rows[:], in_=b1.rearrange("o j (m r) -> (o j m) r", r=NR))
-                make_identity(nc, ident_f[:])
-            elif k == "K":
-                j = a[1]
-                raw = stage.tile([P, 4, L1], BF16, name="raw%d" % j, offset=RAW_SLOT[j], align_bytes=64)
-                nc.sync.dma_start(out=raw[:], in_=k1[j].rearrange("(p t) l -> p t l", t=4))
-                raws[j] = raw
-            elif k == "X":
-                q = a[1]
-                x_sb = stage.tile([P, 2048], BF16, name="x_sb%d" % q, offset=BIG0 + q * 4 * KB, align_bytes=64)
-                nc.sync.dma_start(out=x_sb[:], in_=x_rows[:, q, :])
-                x_parts[q] = x_sb
-            elif k == "BT":
-                g = a[1]
-                pb = psum.tile([P, 4, P], F32, name="pb", tag="bank")
-                for c in range(4):
-                    w = g * 4 + c
-                    nc.tensor.transpose(pb[:, c, :], b_words[:, w:w + 1].to_broadcast([P, P]), ident_f[:])
-                banks[("b", g)] = pb
-            elif k == "BE":
-                g = a[1]
-                engine_copy(a[2], bias_words[:, g * 512:(g + 1) * 512],
-                            banks[("b", g)][:].rearrange("p c g -> p (c g)"))
-            elif k == "XR":
-                q = a[1]
-                xb = stage.tile([P, 2048], BF16, name="xb%d" % q, offset=BIG0 + (16 + 4 * (q % 2)) * KB, align_bytes=64)
-                nc.vector.tensor_copy(
-                    out=xb[:].rearrange("p (c i w) -> p c i w", c=4, i=16),
-                    in_=x_parts[q][:].rearrange("p (i c w) -> p c i w", c=4, i=16),
-                )
-                xbs[q] = xb
-                gxs[q] = stage.tile([P, 2048], BF16, name="gx%d" % q, offset=BIG0 + (24 + 4 * (q % 2)) * KB, align_bytes=64)
-            elif k == "XT":
-                q, h = a[1], a[2]
-                xb32 = xbs[q][:].bitcast(F32)
-                xt = psum.tile([P, 2, 2, P], F32, name="xt", tag="bank")
-                for jj in range(2):
-                    c = 2 * h + jj
-                    for u in range(2):
-                        nc.tensor.transpose(xt[:, jj, u, :], xb32[:, c * 256 + u:(c + 1) * 256:2], ident_f[:])
-                banks[("x", q, h)] = xt
-            elif k == "XE":
-                q, h = a[1], a[2]
-                gx32 = gxs[q][:].bitcast(F32).rearrange("p (j b u) -> p j b u", j=4, u=2)
-                engine_copy(a[3], gx32[:, 2 * h:2 * h + 2], banks[("x", q, h)][:].rearrange("p j u b -> p j b u"))
-            elif k == "XQ":
-                q = a[1]
-                nc.vector.quantize_mx(
-                    out=xcodes[:, q * 512:(q + 1) * 512].bitcast(FP8X4),
-                    scales=xscales[:, q * 512:(q + 1) * 512],
-                    in_=gxs[q][:],
-                )
-            elif k == "U":
-                j, s, eng = a[1], a[2], a[3]
-                grouped = stage.tile([P, 4 * NCOL], BF16, name="grp%d_%d" % (j, s),
-                                     offset=GRP0 + a[4] * 2 * KB, align_bytes=64)
-                if eng == "G":
-                    nc.gpsimd.tensor_scalar(
-                        out=grouped[:].rearrange("p (m r t) -> p m r t", m=NM, t=4),
-                        in0=raws[j][:].rearrange("p t (m s r) -> p s m r t", m=NM, s=NS)[:, s],
-                        scalar1=1.0, scalar2=0.0, op0=MULT, op1=ADD,
-                    )
-                else:
-                    engine_copy(
-                        eng,
-                        grouped[:].rearrange("p (m c i t) -> p m c t i", m=NM, i=4, t=4),
-                        raws[j][:].rearrange("p t (m s c i) -> p s m c t i", m=NM, s=NS, i=4)[:, s],
-                    )
-                pending[(j, s)] = grouped
-            elif k == "Q":
-                j, s = a[1], a[2]
-                grouped = pending[(j, s)]
-                cols = slice(s * NCOL, (s + 1) * NCOL)
-                nc.vector.quantize_mx(
-                    out=kcodes[:, j, cols].bitcast(FP8X4),
-                    scales=kscales[:, j, cols],
-                    in_=grouped[:],
-                )
-            elif k == "MM":
-                s, q = a[1], a[2]
-                ps = psum.tile([P, 512], F32, name="ps", tag="bank")
-                for jj in range(2):
-                    j = 2 * q + jj
+        def quantise(j, s):
+            cols = slice(s * PASS_COLS, (s + 1) * PASS_COLS)
+            nc.vector.quantize_mx(out=k_codes[:, j, cols].bitcast(FP8X4), scales=k_scales[:, j, cols],
+                                  in_=grouped[(j, s)][:])
+
+        def multiply(s):
+            cols = slice(s * PASS_COLS, (s + 1) * PASS_COLS)
+            for q in range(PSUM_BANKS):
+                acc = bank(("y", s, q), [P, BANK_F32])
+                for c in range(BANK_BLOCKS):
+                    j = BANK_BLOCKS * q + c
                     nc.tensor.matmul_mx(
-                        out=ps[:, jj * NCOL:(jj + 1) * NCOL],
-                        lhsT=xcodes[:, j * P:(j + 1) * P].bitcast(FP8X4),
-                        lhsT_scale=xscales[:, j * P:(j + 1) * P],
-                        rhs=kcodes[:, j, s * NCOL:(s + 1) * NCOL].bitcast(FP8X4),
-                        rhs_scale=kscales[:, j, s * NCOL:(s + 1) * NCOL],
+                        out=acc[:, c * PASS_COLS:(c + 1) * PASS_COLS],
+                        lhsT=x_codes[:, j * P:(j + 1) * P].bitcast(FP8X4),
+                        lhsT_scale=x_scales[:, j * P:(j + 1) * P],
+                        rhs=k_codes[:, j, cols].bitcast(FP8X4),
+                        rhs_scale=k_scales[:, j, cols],
                         start=True,
                         stop=True,
                     )
-                banks[("m", s, q)] = ps
-            elif k == "O":
-                s = a[1]
-                osls[s] = stage.tile([P, RS, P], F32, name="osl%d" % s, offset=OSL_OFF[s], align_bytes=64)
-            elif k == "E":
-                s, q, w0, nw = a[1], a[2], a[3], a[4]
-                osl_v = osls[s][:].rearrange("p (w e) g -> p w e g", e=2)
-                nc.vector.tensor_tensor(
-                    out=osl_v[:, w0:w0 + nw, :, q * 16:(q + 1) * 16],
-                    in0=banks[("m", s, q)][:].rearrange("p (g w e) -> p w e g", g=16, e=2)[:, w0:w0 + nw],
-                    in1=bias_v[:, s * 16 + w0:s * 16 + w0 + nw, :, q * 16:(q + 1) * 16],
-                    op=ADD,
-                )
-            elif k == "ES":
-                s, q = a[1], a[2]
-                nc.scalar.copy(
-                    out=osls[s][:, :, q * 16:(q + 1) * 16],
-                    in_=banks[("m", s, q)][:].rearrange("p (g r) -> p r g", g=16),
-                )
-            elif k == "EG":
-                s, q = a[1], a[2]
-                osl_v = osls[s][:].rearrange("p (w e) g -> p w e g", e=2)
-                nc.gpsimd.tensor_tensor(
-                    out=osl_v[:, :, :, q * 16:(q + 1) * 16],
-                    in0=osl_v[:, :, :, q * 16:(q + 1) * 16],
-                    in1=bias_v[:, s * 16:(s + 1) * 16, :, q * 16:(q + 1) * 16],
-                    op=ADD,
-                )
-            elif k == "ST":
-                s, r0, nr = a[1], a[2], a[3]
-                nc.sync.dma_start(out=out[:, s * RS + r0:s * RS + r0 + nr, :], in_=osls[s][:, r0:r0 + nr, :])
+
+        def add_bias_and_store(s, parts):
+            slices[s] = stage.tile([P, SLICE_R, JM], F32, name="slice%d" % s,
+                                   offset=SLICE_BASE[s], align_bytes=64)
+            by_r = slices[s][:].rearrange("p (w e) g -> p w e g", e=2)
+            width = BANK_BLOCKS * M_BLOCKS
+            pairs = SLICE_R // 2 // parts
+            for h in range(parts):
+                w = slice(h * pairs, (h + 1) * pairs)
+                for q in range(PSUM_BANKS):
+                    g = slice(q * width, (q + 1) * width)
+                    nc.vector.tensor_tensor(
+                        out=by_r[:, w, :, g],
+                        in0=banks[("y", s, q)][:].rearrange("p (g w e) -> p w e g", g=width, e=2)[:, w],
+                        in1=bias_by_r[:, s * SLICE_R // 2 + h * pairs:s * SLICE_R // 2 + (h + 1) * pairs, :, g],
+                        op=ADD,
+                    )
+                rows = slice(h * 2 * pairs, (h + 1) * 2 * pairs)
+                nc.sync.dma_start(out=out[:, s * SLICE_R + h * 2 * pairs:s * SLICE_R + (h + 1) * 2 * pairs, :],
+                                  in_=slices[s][:, rows, :])
+
+        nc.sync.dma_start(out=bias_rows[:], in_=b1.rearrange("o j (m r) -> (o j m) r", r=R))
+        make_identity(nc, identity[:])
+        for j in range(RAW_SLOTS):
+            load_weights(j)
+            if j < X_QUARTERS:
+                load_x(j)
+
+        spread = [0]
+        copied = [0]
+
+        def next_bias(limit):
+            if spread[0] < limit:
+                spread_bias(spread[0])
+                spread[0] += 1
+            copy_bias(copied[0])
+            copied[0] += 1
+
+        for g in range(BIAS_AHEAD):
+            spread_bias(g)
+            spread[0] += 1
+        for g in range(2):
+            copy_bias(g)
+            copied[0] += 1
+
+        units = []
+        for j in range(BLOCKS):
+            for s in range(SLICES if j < FIRST_LATE else 2):
+                units.append((j, s))
+        late = []
+        for s in (2, 3):
+            for j in range(FIRST_LATE, BLOCKS):
+                late.append((j, s))
+
+        for n in range(len(units) + SCALAR_LAG + 1):
+            if n < len(units):
+                j, s = units[n]
+                regroup(n, j, s, on_vector(s))
+                if s == SLICES - 1 and j + RAW_SLOTS < BLOCKS:
+                    load_weights(j + RAW_SLOTS)
+            for lag, vector in ((SCALAR_LAG, False), (VECTOR_LAG, True)):
+                if 0 <= n - lag < len(units) and on_vector(units[n - lag][1]) == vector:
+                    quantise(units[n - lag][0], units[n - lag][1])
+            a, step = divmod(n, SLICES)
+            if step == 3 and a < X_QUARTERS:
+                sort_x(a)
+                transpose_x(a)
+            if step == 1 and 1 <= a <= X_QUARTERS:
+                copy_x(a - 1)
+            if step == 1 and 2 <= a <= X_QUARTERS + 1:
+                quantise_x(a - 2)
+            if step == 3 and a >= 1 and copied[0] < EARLY_BIAS_GROUPS:
+                next_bias(EARLY_BIAS_GROUPS)
+
+        half = len(late) // 2
+
+        def late_units(first, last):
+            for i in range(first, last):
+                regroup(len(units) + i, late[i][0], late[i][1], False)
+
+        def late_quantise(first, last):
+            for i in range(first, last):
+                quantise(late[i][0], late[i][1])
+
+        multiply(0)
+        add_bias_and_store(0, 1)
+        late_units(0, half)
+        for g in range(4):
+            next_bias(BIAS_GROUPS)
+        late_quantise(0, 4)
+        multiply(1)
+        add_bias_and_store(1, 1)
+        late_units(half, len(late))
+        for g in range(4):
+            next_bias(BIAS_GROUPS)
+        late_quantise(4, 8)
+        multiply(2)
+        add_bias_and_store(2, 1)
+        late_quantise(8, len(late))
+        multiply(3)
+        add_bias_and_store(3, 2)

@@ -61,7 +61,6 @@ def tile_switchnet_fstar_pa_kernel(tc, x, k1, b1, out):
         keep = ctx.enter_context(tc.tile_pool(name="keep", bufs=1))
         stage = ctx.enter_context(tc.tile_pool(name="stage", bufs=1))
         psum = ctx.enter_context(tc.psum_pool(name="psum", bufs=PSUM_BANKS))
-        ctx.enter_context(tc.manual_schedule())
 
         identity = keep.tile([P, P], F32)
         bias_rows = keep.tile([P, R], BF16)

@@ -17,29 +17,45 @@ K_BLOCK = P * PACK
 COLS = 1024
 M_BLOCKS = 8
 R = 128
+BANK_F32 = 512
+PSUM_BANKS = 8
 SLICE_R = 32
 SLICES = R // SLICE_R
 PASS_COLS = M_BLOCKS * SLICE_R
 JM = BLOCKS * M_BLOCKS
-BANK_F32 = 512
-PSUM_BANKS = 8
 BANK_BLOCKS = BANK_F32 // PASS_COLS
+BANK_JM = BANK_BLOCKS * M_BLOCKS
+
 X_QUARTERS = 4
-BIAS_GROUPS = 16
+QUARTER_BLOCKS = BLOCKS // X_QUARTERS
+WINDOW_ROWS = 16
+QUARTER_VALUES = QUARTER_BLOCKS * K_BLOCK
+BLOCK_WORDS = K_BLOCK // 2
+
+GROUP_WORDS = BANK_F32 // JM
+BIAS_GROUPS = R // (2 * GROUP_WORDS)
+SLICE_GROUPS = BIAS_GROUPS // SLICES
+EARLY_BIAS_GROUPS = 2 * SLICE_GROUPS
+FIRST_SPREAD = 4
+FIRST_COPIED = 2
 
 FIRST_LATE = 11
 VECTOR_LAG = 1
 SCALAR_LAG = 4
-EARLY_BIAS_GROUPS = 8
-BIAS_AHEAD = 4
+EARLY_ADDED = 5
+LATE_AFTER_SLICE_0 = 4
+LATE_AFTER_SLICE_1 = 8
 
 KB = 1024
 RAW_SLOTS = 7
-RAW_BYTES = 8 * KB
+RAW_BYTES = PACK * COLS * 2
 UNIT_SLOTS = 8
-UNIT_BYTES = 2 * KB
+UNIT_BYTES = PACK * PASS_COLS * 2
 UNIT_BASE = RAW_SLOTS * RAW_BYTES
 WIDE_BASE = UNIT_BASE + UNIT_SLOTS * UNIT_BYTES
+QUARTER_BYTES = QUARTER_VALUES * 2
+X_SORTED_BASE = WIDE_BASE + X_QUARTERS * QUARTER_BYTES
+X_GROUPED_BASE = X_SORTED_BASE + 2 * QUARTER_BYTES
 SLICE_BYTES = SLICE_R * JM * 4
 SLICE_BASE = [
     WIDE_BASE,
@@ -61,6 +77,7 @@ def tile_switchnet_fstar_pa_kernel(tc, x, k1, b1, out):
         keep = ctx.enter_context(tc.tile_pool(name="keep", bufs=1))
         stage = ctx.enter_context(tc.tile_pool(name="stage", bufs=1))
         psum = ctx.enter_context(tc.psum_pool(name="psum", bufs=PSUM_BANKS))
+        ctx.enter_context(tc.manual_schedule())
 
         identity = keep.tile([P, P], F32)
         bias_rows = keep.tile([P, R], BF16)
@@ -92,55 +109,55 @@ def tile_switchnet_fstar_pa_kernel(tc, x, k1, b1, out):
                                 offset=(j % RAW_SLOTS) * RAW_BYTES, align_bytes=64)
             nc.sync.dma_start(out=raw[j][:], in_=k1[j].rearrange("(p t) l -> p t l", t=PACK))
 
-        def load_x(a):
-            x_loaded[a] = stage.tile([P, 2048], BF16, name="x_loaded%d" % a,
-                                     offset=WIDE_BASE + a * 4 * KB, align_bytes=64)
-            nc.sync.dma_start(out=x_loaded[a][:], in_=x_quarters[:, a, :])
+        def load_x(quarter):
+            x_loaded[quarter] = stage.tile([P, QUARTER_VALUES], BF16, name="x_loaded%d" % quarter,
+                                           offset=WIDE_BASE + quarter * QUARTER_BYTES, align_bytes=64)
+            nc.sync.dma_start(out=x_loaded[quarter][:], in_=x_quarters[:, quarter, :])
 
-        def spread_bias(g):
-            fanned = bank(("bias", g), [P, 4, JM])
-            for c in range(4):
-                w = 4 * g + c
+        def spread_bias(group):
+            fanned = bank(("bias", group), [P, GROUP_WORDS, JM])
+            for c in range(GROUP_WORDS):
+                w = GROUP_WORDS * group + c
                 nc.tensor.transpose(fanned[:, c, :], bias_row_words[:, w:w + 1].to_broadcast([P, P]), identity[:])
 
-        def copy_bias(g):
-            nc.scalar.copy(out=bias_words[:, g * BANK_F32:(g + 1) * BANK_F32],
-                           in_=banks[("bias", g)][:].rearrange("p c g -> p (c g)"))
+        def copy_bias(group):
+            nc.scalar.copy(out=bias_words[:, group * BANK_F32:(group + 1) * BANK_F32],
+                           in_=banks[("bias", group)][:].rearrange("p c g -> p (c g)"))
 
-        def sort_x(a):
-            x_sorted[a] = stage.tile([P, 2048], BF16, name="x_sorted%d" % a,
-                                     offset=WIDE_BASE + (16 + 4 * (a % 2)) * KB, align_bytes=64)
+        def sort_x(quarter):
+            x_sorted[quarter] = stage.tile([P, QUARTER_VALUES], BF16, name="x_sorted%d" % quarter,
+                                           offset=X_SORTED_BASE + (quarter % 2) * QUARTER_BYTES, align_bytes=64)
             nc.vector.tensor_copy(
-                out=x_sorted[a][:].rearrange("p (c i w) -> p c i w", c=4, i=16),
-                in_=x_loaded[a][:].rearrange("p (i c w) -> p c i w", c=4, i=16),
+                out=x_sorted[quarter][:].rearrange("p (c i v) -> p c i v", c=QUARTER_BLOCKS, i=WINDOW_ROWS),
+                in_=x_loaded[quarter][:].rearrange("p (i c v) -> p c i v", c=QUARTER_BLOCKS, i=WINDOW_ROWS),
             )
-            x_grouped[a] = stage.tile([P, 2048], BF16, name="x_grouped%d" % a,
-                                      offset=WIDE_BASE + (24 + 4 * (a % 2)) * KB, align_bytes=64)
+            x_grouped[quarter] = stage.tile([P, QUARTER_VALUES], BF16, name="x_grouped%d" % quarter,
+                                            offset=X_GROUPED_BASE + (quarter % 2) * QUARTER_BYTES, align_bytes=64)
 
-        def transpose_x(a):
-            words = x_sorted[a][:].bitcast(F32)
-            for h in range(2):
-                turned = bank(("x", a, h), [P, 2, 2, P])
+        def transpose_x(quarter):
+            words = x_sorted[quarter][:].bitcast(F32)
+            for pair in range(QUARTER_BLOCKS // 2):
+                turned = bank(("x", quarter, pair), [P, 2, 2, P])
                 for c in range(2):
-                    first = (2 * h + c) * (K_BLOCK // 2)
+                    first = (2 * pair + c) * BLOCK_WORDS
                     for u in range(2):
                         nc.tensor.transpose(turned[:, c, u, :],
-                                            words[:, first + u:first + K_BLOCK // 2:2], identity[:])
+                                            words[:, first + u:first + BLOCK_WORDS:2], identity[:])
 
-        def copy_x(a):
-            words = x_grouped[a][:].bitcast(F32).rearrange("p (j b u) -> p j b u", j=4, u=2)
-            for h in range(2):
-                nc.scalar.copy(out=words[:, 2 * h:2 * h + 2],
-                               in_=banks[("x", a, h)][:].rearrange("p j u b -> p j b u"))
+        def copy_x(quarter):
+            words = x_grouped[quarter][:].bitcast(F32).rearrange("p (c b u) -> p c b u", c=QUARTER_BLOCKS, u=2)
+            for pair in range(QUARTER_BLOCKS // 2):
+                nc.scalar.copy(out=words[:, 2 * pair:2 * pair + 2],
+                               in_=banks[("x", quarter, pair)][:].rearrange("p c u b -> p c b u"))
 
-        def quantise_x(a):
-            cols = slice(a * 4 * P, (a + 1) * 4 * P)
+        def quantise_x(quarter):
+            cols = slice(quarter * QUARTER_BLOCKS * P, (quarter + 1) * QUARTER_BLOCKS * P)
             nc.vector.quantize_mx(out=x_codes[:, cols].bitcast(FP8X4), scales=x_scales[:, cols],
-                                  in_=x_grouped[a][:])
+                                  in_=x_grouped[quarter][:])
 
-        def regroup(n, j, s, vector):
+        def regroup(step, j, s, vector):
             grouped[(j, s)] = stage.tile([P, PACK * PASS_COLS], BF16, name="unit%d_%d" % (j, s),
-                                         offset=UNIT_BASE + (n % UNIT_SLOTS) * UNIT_BYTES, align_bytes=64)
+                                         offset=UNIT_BASE + (step % UNIT_SLOTS) * UNIT_BYTES, align_bytes=64)
             dst = grouped[(j, s)][:].rearrange("p (m c i t) -> p m c t i", m=M_BLOCKS, i=4, t=PACK)
             src = raw[j][:].rearrange("p t (m s c i) -> p s m c t i", m=M_BLOCKS, s=SLICES, i=4)[:, s]
             if vector:
@@ -153,9 +170,9 @@ def tile_switchnet_fstar_pa_kernel(tc, x, k1, b1, out):
             nc.vector.quantize_mx(out=k_codes[:, j, cols].bitcast(FP8X4), scales=k_scales[:, j, cols],
                                   in_=grouped[(j, s)][:])
 
-        def multiply(s):
+        def multiply(s, first_bank=0, last_bank=PSUM_BANKS):
             cols = slice(s * PASS_COLS, (s + 1) * PASS_COLS)
-            for q in range(PSUM_BANKS):
+            for q in range(first_bank, last_bank):
                 acc = bank(("y", s, q), [P, BANK_F32])
                 for c in range(BANK_BLOCKS):
                     j = BANK_BLOCKS * q + c
@@ -169,25 +186,34 @@ def tile_switchnet_fstar_pa_kernel(tc, x, k1, b1, out):
                         stop=True,
                     )
 
-        def add_bias_and_store(s, parts):
+        def new_slice(s):
             slices[s] = stage.tile([P, SLICE_R, JM], F32, name="slice%d" % s,
                                    offset=SLICE_BASE[s], align_bytes=64)
+
+        def add_bias(s, part, parts, first_bank, last_bank):
             by_r = slices[s][:].rearrange("p (w e) g -> p w e g", e=2)
-            width = BANK_BLOCKS * M_BLOCKS
             pairs = SLICE_R // 2 // parts
-            for h in range(parts):
-                w = slice(h * pairs, (h + 1) * pairs)
-                for q in range(PSUM_BANKS):
-                    g = slice(q * width, (q + 1) * width)
-                    nc.vector.tensor_tensor(
-                        out=by_r[:, w, :, g],
-                        in0=banks[("y", s, q)][:].rearrange("p (g w e) -> p w e g", g=width, e=2)[:, w],
-                        in1=bias_by_r[:, s * SLICE_R // 2 + h * pairs:s * SLICE_R // 2 + (h + 1) * pairs, :, g],
-                        op=ADD,
-                    )
-                rows = slice(h * 2 * pairs, (h + 1) * 2 * pairs)
-                nc.sync.dma_start(out=out[:, s * SLICE_R + h * 2 * pairs:s * SLICE_R + (h + 1) * 2 * pairs, :],
-                                  in_=slices[s][:, rows, :])
+            in_slice = slice(part * pairs, (part + 1) * pairs)
+            in_bias = slice(s * SLICE_R // 2 + part * pairs, s * SLICE_R // 2 + (part + 1) * pairs)
+            for q in range(first_bank, last_bank):
+                jm = slice(q * BANK_JM, (q + 1) * BANK_JM)
+                nc.vector.tensor_tensor(
+                    out=by_r[:, in_slice, :, jm],
+                    in0=banks[("y", s, q)][:].rearrange("p (g w e) -> p w e g", g=BANK_JM, e=2)[:, in_slice],
+                    in1=bias_by_r[:, in_bias, :, jm],
+                    op=ADD,
+                )
+
+        def store(s, part, parts):
+            rows = SLICE_R // parts
+            nc.sync.dma_start(out=out[:, s * SLICE_R + part * rows:s * SLICE_R + (part + 1) * rows, :],
+                              in_=slices[s][:, part * rows:(part + 1) * rows, :])
+
+        def add_bias_and_store(s, parts):
+            new_slice(s)
+            for part in range(parts):
+                add_bias(s, part, parts, 0, PSUM_BANKS)
+                store(s, part, parts)
 
         nc.sync.dma_start(out=bias_rows[:], in_=b1.rearrange("o j (m r) -> (o j m) r", r=R))
         make_identity(nc, identity[:])
@@ -199,19 +225,18 @@ def tile_switchnet_fstar_pa_kernel(tc, x, k1, b1, out):
         spread = [0]
         copied = [0]
 
-        def next_bias(limit):
-            if spread[0] < limit:
-                spread_bias(spread[0])
-                spread[0] += 1
+        def next_spread():
+            spread_bias(spread[0])
+            spread[0] += 1
+
+        def next_copy():
             copy_bias(copied[0])
             copied[0] += 1
 
-        for g in range(BIAS_AHEAD):
-            spread_bias(g)
-            spread[0] += 1
-        for g in range(2):
-            copy_bias(g)
-            copied[0] += 1
+        for group in range(FIRST_SPREAD):
+            next_spread()
+        for group in range(FIRST_COPIED):
+            next_copy()
 
         units = []
         for j in range(BLOCKS):
@@ -222,27 +247,34 @@ def tile_switchnet_fstar_pa_kernel(tc, x, k1, b1, out):
             for j in range(FIRST_LATE, BLOCKS):
                 late.append((j, s))
 
-        for n in range(len(units) + SCALAR_LAG + 1):
-            if n < len(units):
-                j, s = units[n]
-                regroup(n, j, s, on_vector(s))
+        for step in range(len(units) + SCALAR_LAG + 1):
+            if step < len(units):
+                j, s = units[step]
+                regroup(step, j, s, on_vector(s))
                 if s == SLICES - 1 and j + RAW_SLOTS < BLOCKS:
                     load_weights(j + RAW_SLOTS)
             for lag, vector in ((SCALAR_LAG, False), (VECTOR_LAG, True)):
-                if 0 <= n - lag < len(units) and on_vector(units[n - lag][1]) == vector:
-                    quantise(units[n - lag][0], units[n - lag][1])
-            a, step = divmod(n, SLICES)
-            if step == 3 and a < X_QUARTERS:
-                sort_x(a)
-                transpose_x(a)
-            if step == 1 and 1 <= a <= X_QUARTERS:
-                copy_x(a - 1)
-            if step == 1 and 2 <= a <= X_QUARTERS + 1:
-                quantise_x(a - 2)
-            if step == 3 and a >= 1 and copied[0] < EARLY_BIAS_GROUPS:
-                next_bias(EARLY_BIAS_GROUPS)
-
-        half = len(late) // 2
+                if 0 <= step - lag < len(units) and on_vector(units[step - lag][1]) == vector:
+                    quantise(units[step - lag][0], units[step - lag][1])
+            block, place = divmod(step, SLICES)
+            if place == 3 and block < X_QUARTERS:
+                sort_x(block)
+                transpose_x(block)
+            if place == 1 and 1 <= block <= X_QUARTERS:
+                copy_x(block - 1)
+            if place == 1 and 2 <= block <= X_QUARTERS + 1:
+                quantise_x(block - 2)
+            if step < len(units) and units[step][0] >= FIRST_LATE and units[step][1] == 1:
+                i = units[step][0] - FIRST_LATE
+                if i == 0:
+                    multiply(0, 0, EARLY_ADDED)
+                    new_slice(0)
+                if 2 * i < EARLY_ADDED:
+                    add_bias(0, 0, 1, 2 * i, min(2 * i + 2, EARLY_ADDED))
+            if place == 3 and block >= 1 and copied[0] < EARLY_BIAS_GROUPS:
+                if spread[0] < EARLY_BIAS_GROUPS:
+                    next_spread()
+                next_copy()
 
         def late_units(first, last):
             for i in range(first, last):
@@ -252,20 +284,24 @@ def tile_switchnet_fstar_pa_kernel(tc, x, k1, b1, out):
             for i in range(first, last):
                 quantise(late[i][0], late[i][1])
 
-        multiply(0)
-        add_bias_and_store(0, 1)
-        late_units(0, half)
-        for g in range(4):
-            next_bias(BIAS_GROUPS)
-        late_quantise(0, 4)
+        def late_bias():
+            for group in range(SLICE_GROUPS):
+                next_spread()
+                next_copy()
+
+        multiply(0, EARLY_ADDED, PSUM_BANKS)
+        add_bias(0, 0, 1, EARLY_ADDED, PSUM_BANKS)
+        store(0, 0, 1)
+        late_units(0, len(late) // 2)
+        late_bias()
+        late_quantise(0, LATE_AFTER_SLICE_0)
         multiply(1)
         add_bias_and_store(1, 1)
-        late_units(half, len(late))
-        for g in range(4):
-            next_bias(BIAS_GROUPS)
-        late_quantise(4, 8)
+        late_units(len(late) // 2, len(late))
+        late_bias()
+        late_quantise(LATE_AFTER_SLICE_0, LATE_AFTER_SLICE_1)
         multiply(2)
         add_bias_and_store(2, 1)
-        late_quantise(8, len(late))
+        late_quantise(LATE_AFTER_SLICE_1, len(late))
         multiply(3)
         add_bias_and_store(3, 2)

@@ -9,6 +9,7 @@ U32 = mybir.dt.uint32
 U8 = mybir.dt.uint8
 FP8X4 = mybir.dt.float8_e4m3fn_x4
 ADD = mybir.AluOpType.add
+MULT = mybir.AluOpType.mult
 
 P = 128
 PACK = 4
@@ -276,9 +277,25 @@ def tile_switchnet_fstar_pa_kernel(tc, x, k1, b1, out):
                     next_spread()
                 next_copy()
 
+        late_step = {}
+
         def late_units(first, last):
             for i in range(first, last):
-                regroup(len(units) + i, late[i][0], late[i][1], False)
+                late_step[i] = len(units) + i
+                regroup(late_step[i], late[i][0], late[i][1], False)
+
+        def late_units_on_gpsimd(first, last, newest_read):
+            for n, i in enumerate(range(first, last)):
+                late_step[i] = late_step[newest_read - n]
+                j, s = late[i]
+                grouped[(j, s)] = stage.tile([P, PACK * PASS_COLS], BF16, name="unit%d_%d" % (j, s),
+                                             offset=UNIT_BASE + (late_step[i] % UNIT_SLOTS) * UNIT_BYTES,
+                                             align_bytes=64)
+                nc.gpsimd.tensor_scalar(
+                    out=grouped[(j, s)][:].rearrange("p (m r t) -> p m r t", m=M_BLOCKS, t=PACK),
+                    in0=raw[j][:].rearrange("p t (m s r) -> p s m r t", m=M_BLOCKS, s=SLICES)[:, s],
+                    scalar1=1.0, scalar2=0.0, op0=MULT, op1=ADD,
+                )
 
         def late_quantise(first, last):
             for i in range(first, last):
@@ -295,11 +312,12 @@ def tile_switchnet_fstar_pa_kernel(tc, x, k1, b1, out):
         late_units(0, len(late) // 2)
         late_bias()
         late_quantise(0, LATE_AFTER_SLICE_0)
+        late_units_on_gpsimd(len(late) // 2, LATE_AFTER_SLICE_1, LATE_AFTER_SLICE_0 - 1)
         multiply(1)
         add_bias_and_store(1, 1)
-        late_units(len(late) // 2, len(late))
         late_bias()
         late_quantise(LATE_AFTER_SLICE_0, LATE_AFTER_SLICE_1)
+        late_units_on_gpsimd(LATE_AFTER_SLICE_1, len(late), LATE_AFTER_SLICE_1 - 1)
         multiply(2)
         add_bias_and_store(2, 1)
         late_quantise(LATE_AFTER_SLICE_1, len(late))

@@ -22,10 +22,16 @@ BANK_F32 = 512
 PSUM_BANKS = 8
 SLICE_R = 32
 SLICES = R // SLICE_R
-PASS_COLS = M_BLOCKS * SLICE_R
+UNIT_COLS = M_BLOCKS * SLICE_R
+RUN = 4
+PIECE_R = 16
+PIECES = R // PIECE_R
+SLICE_PIECES = PIECES // SLICES
+PASS_COLS = M_BLOCKS * PIECE_R
 JM = BLOCKS * M_BLOCKS
 BANK_BLOCKS = BANK_F32 // PASS_COLS
 BANK_JM = BANK_BLOCKS * M_BLOCKS
+PIECE_BANKS = BLOCKS // BANK_BLOCKS
 
 X_QUARTERS = 4
 QUARTER_BLOCKS = BLOCKS // X_QUARTERS
@@ -43,7 +49,7 @@ FIRST_COPIED = 2
 FIRST_LATE = 11
 VECTOR_LAG = 1
 SCALAR_LAG = 4
-EARLY_ADDED = 5
+EARLY_BANKS = 2
 LATE_AFTER_SLICE_0 = 4
 LATE_AFTER_SLICE_1 = 8
 
@@ -51,13 +57,14 @@ KB = 1024
 RAW_SLOTS = 7
 RAW_BYTES = PACK * COLS * 2
 UNIT_SLOTS = 8
-UNIT_BYTES = PACK * PASS_COLS * 2
+UNIT_BYTES = PACK * UNIT_COLS * 2
 UNIT_BASE = RAW_SLOTS * RAW_BYTES
 WIDE_BASE = UNIT_BASE + UNIT_SLOTS * UNIT_BYTES
 QUARTER_BYTES = QUARTER_VALUES * 2
 X_SORTED_BASE = WIDE_BASE + X_QUARTERS * QUARTER_BYTES
 X_GROUPED_BASE = X_SORTED_BASE + 2 * QUARTER_BYTES
 SLICE_BYTES = SLICE_R * JM * 4
+PIECE_BYTES = PIECE_R * JM * 4
 SLICE_BASE = [
     WIDE_BASE,
     WIDE_BASE + SLICE_BYTES,
@@ -99,7 +106,7 @@ def tile_switchnet_fstar_pa_kernel(tc, x, k1, b1, out):
         x_sorted = {}
         x_grouped = {}
         banks = {}
-        slices = {}
+        pieces = {}
 
         def bank(key, shape):
             banks[key] = psum.tile(shape, F32, name="bank", tag="bank")
@@ -157,24 +164,25 @@ def tile_switchnet_fstar_pa_kernel(tc, x, k1, b1, out):
                                   in_=x_grouped[quarter][:])
 
         def regroup(step, j, s, vector):
-            grouped[(j, s)] = stage.tile([P, PACK * PASS_COLS], BF16, name="unit%d_%d" % (j, s),
+            grouped[(j, s)] = stage.tile([P, PACK * UNIT_COLS], BF16, name="unit%d_%d" % (j, s),
                                          offset=UNIT_BASE + (step % UNIT_SLOTS) * UNIT_BYTES, align_bytes=64)
-            dst = grouped[(j, s)][:].rearrange("p (m c i t) -> p m c t i", m=M_BLOCKS, i=4, t=PACK)
-            src = raw[j][:].rearrange("p t (m s c i) -> p s m c t i", m=M_BLOCKS, s=SLICES, i=4)[:, s]
-            if vector:
-                nc.vector.tensor_copy(out=dst, in_=src)
-            else:
-                nc.scalar.copy(out=dst, in_=src)
+            by_piece = grouped[(j, s)][:].rearrange("p (h m c i t) -> p h m c t i", h=SLICE_PIECES, m=M_BLOCKS, i=RUN, t=PACK)
+            raw_by_piece = raw[j][:].rearrange("p t (m s h c i) -> p s h m c t i", m=M_BLOCKS, s=SLICES, h=SLICE_PIECES, i=RUN)
+            for h in range(SLICE_PIECES):
+                if vector:
+                    nc.vector.tensor_copy(out=by_piece[:, h], in_=raw_by_piece[:, s, h])
+                else:
+                    nc.scalar.copy(out=by_piece[:, h], in_=raw_by_piece[:, s, h])
 
         def quantise(j, s):
-            cols = slice(s * PASS_COLS, (s + 1) * PASS_COLS)
+            cols = slice(s * UNIT_COLS, (s + 1) * UNIT_COLS)
             nc.vector.quantize_mx(out=k_codes[:, j, cols].bitcast(FP8X4), scales=k_scales[:, j, cols],
                                   in_=grouped[(j, s)][:])
 
-        def multiply(s, first_bank=0, last_bank=PSUM_BANKS):
-            cols = slice(s * PASS_COLS, (s + 1) * PASS_COLS)
+        def multiply(h, first_bank=0, last_bank=PIECE_BANKS):
+            cols = slice(h * PASS_COLS, (h + 1) * PASS_COLS)
             for q in range(first_bank, last_bank):
-                acc = bank(("y", s, q), [P, BANK_F32])
+                acc = bank(("y", h, q), [P, BANK_F32])
                 for c in range(BANK_BLOCKS):
                     j = BANK_BLOCKS * q + c
                     nc.tensor.matmul_mx(
@@ -187,34 +195,39 @@ def tile_switchnet_fstar_pa_kernel(tc, x, k1, b1, out):
                         stop=True,
                     )
 
-        def new_slice(s):
-            slices[s] = stage.tile([P, SLICE_R, JM], F32, name="slice%d" % s,
-                                   offset=SLICE_BASE[s], align_bytes=64)
+        def new_piece(h):
+            pieces[h] = stage.tile([P, PIECE_R, JM], F32, name="piece%d" % h,
+                                   offset=SLICE_BASE[h // SLICE_PIECES] + (h % SLICE_PIECES) * PIECE_BYTES,
+                                   align_bytes=64)
 
-        def add_bias(s, part, parts, first_bank, last_bank):
-            by_r = slices[s][:].rearrange("p (w e) g -> p w e g", e=2)
-            pairs = SLICE_R // 2 // parts
-            in_slice = slice(part * pairs, (part + 1) * pairs)
-            in_bias = slice(s * SLICE_R // 2 + part * pairs, s * SLICE_R // 2 + (part + 1) * pairs)
+        def add_bias(h, first_bank, last_bank, part=0, parts=1):
+            by_r = pieces[h][:].rearrange("p (w e) g -> p w e g", e=2)
+            pairs = PIECE_R // 2 // parts
+            in_piece = slice(part * pairs, (part + 1) * pairs)
+            in_bias = slice(h * PIECE_R // 2 + part * pairs, h * PIECE_R // 2 + (part + 1) * pairs)
             for q in range(first_bank, last_bank):
                 jm = slice(q * BANK_JM, (q + 1) * BANK_JM)
                 nc.vector.tensor_tensor(
-                    out=by_r[:, in_slice, :, jm],
-                    in0=banks[("y", s, q)][:].rearrange("p (g w e) -> p w e g", g=BANK_JM, e=2)[:, in_slice],
+                    out=by_r[:, in_piece, :, jm],
+                    in0=banks[("y", h, q)][:].rearrange("p (g w e) -> p w e g", g=BANK_JM, e=2)[:, in_piece],
                     in1=bias_by_r[:, in_bias, :, jm],
                     op=ADD,
                 )
 
-        def store(s, part, parts):
-            rows = SLICE_R // parts
-            nc.sync.dma_start(out=out[:, s * SLICE_R + part * rows:s * SLICE_R + (part + 1) * rows, :],
-                              in_=slices[s][:, part * rows:(part + 1) * rows, :])
+        def store(h, part=0, parts=1):
+            rows = PIECE_R // parts
+            nc.sync.dma_start(out=out[:, h * PIECE_R + part * rows:h * PIECE_R + (part + 1) * rows, :],
+                              in_=pieces[h][:, part * rows:(part + 1) * rows, :])
 
-        def add_bias_and_store(s, parts):
-            new_slice(s)
-            for part in range(parts):
-                add_bias(s, part, parts, 0, PSUM_BANKS)
-                store(s, part, parts)
+        def finish_slice(s):
+            for h in range(s * SLICE_PIECES, (s + 1) * SLICE_PIECES):
+                multiply(h)
+            for h in range(s * SLICE_PIECES, (s + 1) * SLICE_PIECES):
+                new_piece(h)
+                halves = 2 if h == PIECES - 1 else 1
+                for part in range(halves):
+                    add_bias(h, 0, PIECE_BANKS, part, halves)
+                    store(h, part, halves)
 
         nc.sync.dma_start(out=bias_rows[:], in_=b1.rearrange("o j (m r) -> (o j m) r", r=R))
         make_identity(nc, identity[:])
@@ -268,10 +281,12 @@ def tile_switchnet_fstar_pa_kernel(tc, x, k1, b1, out):
             if step < len(units) and units[step][0] >= FIRST_LATE and units[step][1] == 1:
                 i = units[step][0] - FIRST_LATE
                 if i == 0:
-                    multiply(0, 0, EARLY_ADDED)
-                    new_slice(0)
-                if 2 * i < EARLY_ADDED:
-                    add_bias(0, 0, 1, 2 * i, min(2 * i + 2, EARLY_ADDED))
+                    for h in range(SLICE_PIECES):
+                        multiply(h, 0, EARLY_BANKS)
+                        new_piece(h)
+                if i < EARLY_BANKS:
+                    for h in range(SLICE_PIECES):
+                        add_bias(h, i, i + 1)
             if place == 3 and block >= 1 and copied[0] < EARLY_BIAS_GROUPS:
                 if spread[0] < EARLY_BIAS_GROUPS:
                     next_spread()
@@ -288,14 +303,14 @@ def tile_switchnet_fstar_pa_kernel(tc, x, k1, b1, out):
             for n, i in enumerate(range(first, last)):
                 late_step[i] = late_step[newest_read - n]
                 j, s = late[i]
-                grouped[(j, s)] = stage.tile([P, PACK * PASS_COLS], BF16, name="unit%d_%d" % (j, s),
+                grouped[(j, s)] = stage.tile([P, PACK * UNIT_COLS], BF16, name="unit%d_%d" % (j, s),
                                              offset=UNIT_BASE + (late_step[i] % UNIT_SLOTS) * UNIT_BYTES,
                                              align_bytes=64)
-                nc.gpsimd.tensor_scalar(
-                    out=grouped[(j, s)][:].rearrange("p (m r t) -> p m r t", m=M_BLOCKS, t=PACK),
-                    in0=raw[j][:].rearrange("p t (m s r) -> p s m r t", m=M_BLOCKS, s=SLICES)[:, s],
-                    scalar1=1.0, scalar2=0.0, op0=MULT, op1=ADD,
-                )
+                by_piece = grouped[(j, s)][:].rearrange("p (h m r t) -> p h m r t", h=SLICE_PIECES, m=M_BLOCKS, t=PACK)
+                raw_by_piece = raw[j][:].rearrange("p t (m s h r) -> p s h m r t", m=M_BLOCKS, s=SLICES, h=SLICE_PIECES)
+                for h in range(SLICE_PIECES):
+                    nc.gpsimd.tensor_scalar(out=by_piece[:, h], in0=raw_by_piece[:, s, h],
+                                            scalar1=1.0, scalar2=0.0, op0=MULT, op1=ADD)
 
         def late_quantise(first, last):
             for i in range(first, last):
@@ -306,20 +321,19 @@ def tile_switchnet_fstar_pa_kernel(tc, x, k1, b1, out):
                 next_spread()
                 next_copy()
 
-        multiply(0, EARLY_ADDED, PSUM_BANKS)
-        add_bias(0, 0, 1, EARLY_ADDED, PSUM_BANKS)
-        store(0, 0, 1)
+        for h in range(SLICE_PIECES):
+            multiply(h, EARLY_BANKS, PIECE_BANKS)
+        for h in range(SLICE_PIECES):
+            add_bias(h, EARLY_BANKS, PIECE_BANKS)
+            store(h)
         late_units(0, len(late) // 2)
         late_bias()
         late_quantise(0, LATE_AFTER_SLICE_0)
         late_units_on_gpsimd(len(late) // 2, LATE_AFTER_SLICE_1, LATE_AFTER_SLICE_0 - 1)
-        multiply(1)
-        add_bias_and_store(1, 1)
+        finish_slice(1)
         late_bias()
         late_quantise(LATE_AFTER_SLICE_0, LATE_AFTER_SLICE_1)
         late_units_on_gpsimd(LATE_AFTER_SLICE_1, len(late), LATE_AFTER_SLICE_1 - 1)
-        multiply(2)
-        add_bias_and_store(2, 1)
+        finish_slice(2)
         late_quantise(LATE_AFTER_SLICE_1, len(late))
-        multiply(3)
-        add_bias_and_store(3, 2)
+        finish_slice(3)

@@ -38,6 +38,7 @@ QUARTER_BLOCKS = BLOCKS // X_QUARTERS
 WINDOW_ROWS = 16
 QUARTER_VALUES = QUARTER_BLOCKS * K_BLOCK
 BLOCK_WORDS = K_BLOCK // 2
+X_BEHIND = 2
 
 GROUP_WORDS = BANK_F32 // JM
 BIAS_GROUPS = R // (2 * GROUP_WORDS)
@@ -233,8 +234,8 @@ def tile_switchnet_fstar_pa_kernel(tc, x, k1, b1, out):
         make_identity(nc, identity[:])
         for j in range(RAW_SLOTS):
             load_weights(j)
-            if j < X_QUARTERS:
-                load_x(j)
+            if 0 <= j - X_BEHIND < X_QUARTERS:
+                load_x(j - X_BEHIND)
 
         spread = [0]
         copied = [0]
@@ -271,13 +272,14 @@ def tile_switchnet_fstar_pa_kernel(tc, x, k1, b1, out):
                 if 0 <= step - lag < len(units) and on_vector(units[step - lag][1]) == vector:
                     quantise(units[step - lag][0], units[step - lag][1])
             block, place = divmod(step, SLICES)
-            if place == 3 and block < X_QUARTERS:
-                sort_x(block)
-                transpose_x(block)
-            if place == 1 and 1 <= block <= X_QUARTERS:
-                copy_x(block - 1)
-            if place == 1 and 2 <= block <= X_QUARTERS + 1:
-                quantise_x(block - 2)
+            quarter = block - X_BEHIND
+            if place == 3 and 0 <= quarter < X_QUARTERS:
+                sort_x(quarter)
+                transpose_x(quarter)
+            if place == 1 and 1 <= quarter <= X_QUARTERS:
+                copy_x(quarter - 1)
+            if place == 1 and 2 <= quarter <= X_QUARTERS + 1:
+                quantise_x(quarter - 2)
             if step < len(units) and units[step][0] >= FIRST_LATE and units[step][1] == 1:
                 i = units[step][0] - FIRST_LATE
                 if i == 0:

@@ -47,15 +47,15 @@ EARLY_BIAS_GROUPS = 2 * SLICE_GROUPS
 FIRST_SPREAD = 4
 FIRST_COPIED = 2
 
-FIRST_LATE = 11
+FIRST_LATE = 8
+GPSIMD_FIRST = 2
+GPSIMD_LAST = 3
+FILL_BEHIND = 3
+ROUND_BLOCKS = (9, 12)
 VECTOR_LAG = 1
 SCALAR_LAG = 4
-EARLY_BANKS = 2
-LATE_AFTER_SLICE_0 = 4
-LATE_AFTER_SLICE_1 = 8
 
-KB = 1024
-RAW_SLOTS = 7
+RAW_SLOTS = 10
 RAW_BYTES = PACK * COLS * 2
 UNIT_SLOTS = 8
 UNIT_BYTES = PACK * UNIT_COLS * 2
@@ -64,20 +64,14 @@ WIDE_BASE = UNIT_BASE + UNIT_SLOTS * UNIT_BYTES
 QUARTER_BYTES = QUARTER_VALUES * 2
 X_SORTED_BASE = WIDE_BASE + X_QUARTERS * QUARTER_BYTES
 X_GROUPED_BASE = X_SORTED_BASE + 2 * QUARTER_BYTES
-SLICE_BYTES = SLICE_R * JM * 4
 PIECE_BYTES = PIECE_R * JM * 4
-SLICE_BASE = [
-    WIDE_BASE,
-    WIDE_BASE + SLICE_BYTES,
-    ((FIRST_LATE - 2) % RAW_SLOTS) * RAW_BYTES,
-    WIDE_BASE,
-]
+PIECE_SLOTS = 4
 
 FLOPS = 2 * P * K_BLOCK * COLS * BLOCKS
 
 
-def on_vector(s):
-    return s % 2 == 0
+def on_vector(j, s):
+    return s % 2 == 0 and (j < FIRST_LATE or s < 2)
 
 
 def tile_switchnet_fstar_pa_kernel(tc, x, k1, b1, out):
@@ -90,7 +84,7 @@ def tile_switchnet_fstar_pa_kernel(tc, x, k1, b1, out):
 
         identity = keep.tile([P, P], F32)
         bias_rows = keep.tile([P, R], BF16)
-        bias = keep.tile([P, R * JM], BF16)
+        bias = keep.tile([P, R * JM // 2], BF16)
         k_codes = keep.tile([P, BLOCKS, COLS], U32, align_bytes=64)
         k_scales = keep.tile([P, BLOCKS, COLS], U8, align_bytes=64)
         x_codes = keep.tile([P, BLOCKS * P], U32, align_bytes=64)
@@ -103,6 +97,7 @@ def tile_switchnet_fstar_pa_kernel(tc, x, k1, b1, out):
 
         raw = {}
         grouped = {}
+        slot_of = {}
         x_loaded = {}
         x_sorted = {}
         x_grouped = {}
@@ -130,7 +125,8 @@ def tile_switchnet_fstar_pa_kernel(tc, x, k1, b1, out):
                 nc.tensor.transpose(fanned[:, c, :], bias_row_words[:, w:w + 1].to_broadcast([P, P]), identity[:])
 
         def copy_bias(group):
-            nc.scalar.copy(out=bias_words[:, group * BANK_F32:(group + 1) * BANK_F32],
+            place = group % EARLY_BIAS_GROUPS
+            nc.scalar.copy(out=bias_words[:, place * BANK_F32:(place + 1) * BANK_F32],
                            in_=banks[("bias", group)][:].rearrange("p c g -> p (c g)"))
 
         def sort_x(quarter):
@@ -164,9 +160,16 @@ def tile_switchnet_fstar_pa_kernel(tc, x, k1, b1, out):
             nc.vector.quantize_mx(out=x_codes[:, cols].bitcast(FP8X4), scales=x_scales[:, cols],
                                   in_=x_grouped[quarter][:])
 
-        def regroup(step, j, s, vector):
+        free_slots = list(range(UNIT_SLOTS))
+
+        def new_unit(j, s, slot):
+            free_slots.remove(slot)
+            slot_of[(j, s)] = slot
             grouped[(j, s)] = stage.tile([P, PACK * UNIT_COLS], BF16, name="unit%d_%d" % (j, s),
-                                         offset=UNIT_BASE + (step % UNIT_SLOTS) * UNIT_BYTES, align_bytes=64)
+                                         offset=UNIT_BASE + slot * UNIT_BYTES, align_bytes=64)
+
+        def regroup(j, s, vector):
+            new_unit(j, s, free_slots[0])
             by_piece = grouped[(j, s)][:].rearrange("p (h m c i t) -> p h m c t i", h=SLICE_PIECES, m=M_BLOCKS, i=RUN, t=PACK)
             raw_by_piece = raw[j][:].rearrange("p t (m s h c i) -> p s h m c t i", m=M_BLOCKS, s=SLICES, h=SLICE_PIECES, i=RUN)
             for h in range(SLICE_PIECES):
@@ -179,6 +182,7 @@ def tile_switchnet_fstar_pa_kernel(tc, x, k1, b1, out):
             cols = slice(s * UNIT_COLS, (s + 1) * UNIT_COLS)
             nc.vector.quantize_mx(out=k_codes[:, j, cols].bitcast(FP8X4), scales=k_scales[:, j, cols],
                                   in_=grouped[(j, s)][:])
+            free_slots.append(slot_of[(j, s)])
 
         def multiply(h, first_bank=0, last_bank=PIECE_BANKS):
             cols = slice(h * PASS_COLS, (h + 1) * PASS_COLS)
@@ -198,14 +202,15 @@ def tile_switchnet_fstar_pa_kernel(tc, x, k1, b1, out):
 
         def new_piece(h):
             pieces[h] = stage.tile([P, PIECE_R, JM], F32, name="piece%d" % h,
-                                   offset=SLICE_BASE[h // SLICE_PIECES] + (h % SLICE_PIECES) * PIECE_BYTES,
+                                   offset=WIDE_BASE + (h % PIECE_SLOTS) * PIECE_BYTES,
                                    align_bytes=64)
 
         def add_bias(h, first_bank, last_bank, part=0, parts=1):
             by_r = pieces[h][:].rearrange("p (w e) g -> p w e g", e=2)
             pairs = PIECE_R // 2 // parts
             in_piece = slice(part * pairs, (part + 1) * pairs)
-            in_bias = slice(h * PIECE_R // 2 + part * pairs, h * PIECE_R // 2 + (part + 1) * pairs)
+            first_pair = (h % PIECE_SLOTS) * PIECE_R // 2
+            in_bias = slice(first_pair + part * pairs, first_pair + (part + 1) * pairs)
             for q in range(first_bank, last_bank):
                 jm = slice(q * BANK_JM, (q + 1) * BANK_JM)
                 nc.vector.tensor_tensor(
@@ -219,16 +224,6 @@ def tile_switchnet_fstar_pa_kernel(tc, x, k1, b1, out):
             rows = PIECE_R // parts
             nc.sync.dma_start(out=out[:, h * PIECE_R + part * rows:h * PIECE_R + (part + 1) * rows, :],
                               in_=pieces[h][:, part * rows:(part + 1) * rows, :])
-
-        def finish_slice(s):
-            for h in range(s * SLICE_PIECES, (s + 1) * SLICE_PIECES):
-                multiply(h)
-            for h in range(s * SLICE_PIECES, (s + 1) * SLICE_PIECES):
-                new_piece(h)
-                halves = 2 if h == PIECES - 1 else 1
-                for part in range(halves):
-                    add_bias(h, 0, PIECE_BANKS, part, halves)
-                    store(h, part, halves)
 
         nc.sync.dma_start(out=bias_rows[:], in_=b1.rearrange("o j (m r) -> (o j m) r", r=R))
         make_identity(nc, identity[:])
@@ -253,23 +248,62 @@ def tile_switchnet_fstar_pa_kernel(tc, x, k1, b1, out):
         for group in range(FIRST_COPIED):
             next_copy()
 
+        def regroup_on_gpsimd(j, s):
+            new_unit(j, s, free_slots[-1])
+            by_piece = grouped[(j, s)][:].rearrange("p (h m r t) -> p h m r t", h=SLICE_PIECES, m=M_BLOCKS, t=PACK)
+            raw_by_piece = raw[j][:].rearrange("p t (m s h r) -> p s h m r t", m=M_BLOCKS, s=SLICES, h=SLICE_PIECES)
+            for h in range(SLICE_PIECES):
+                nc.gpsimd.tensor_scalar(out=by_piece[:, h], in0=raw_by_piece[:, s, h],
+                                        scalar1=1.0, scalar2=0.0, op0=MULT, op1=ADD)
+
+        def multiply_banks(tasks):
+            for h, q in tasks:
+                multiply(h, q, q + 1)
+
+        riding = []
+        added = {}
+
+        def add_round(tasks, ride, after_ride=(), parts=1):
+            for j, s in riding:
+                quantise(j, s)
+            riding.clear()
+            for j, s in ride:
+                regroup_on_gpsimd(j, s)
+                riding.append((j, s))
+            multiply_banks(after_ride)
+            for part in range(parts):
+                for h, q in tasks:
+                    if h not in pieces:
+                        new_piece(h)
+                    add_bias(h, q, q + 1, part, parts)
+                    added[h] = added.get(h, 0) + 1
+                    if added[h] % PIECE_BANKS == 0:
+                        store(h, part, parts)
+
+        def bias_groups(count):
+            for group in range(count):
+                next_spread()
+                next_copy()
+
+        def banks_of(first_piece, last_piece, first_bank, last_bank):
+            return [(h, q) for h in range(first_piece, last_piece) for q in range(first_bank, last_bank)]
+
+        first_gpsimd_last = BLOCKS - GPSIMD_LAST
         units = []
         for j in range(BLOCKS):
             for s in range(SLICES if j < FIRST_LATE else 2):
                 units.append((j, s))
-        late = []
-        for s in (2, 3):
-            for j in range(FIRST_LATE, BLOCKS):
-                late.append((j, s))
+            if FIRST_LATE + GPSIMD_FIRST <= j - FILL_BEHIND < first_gpsimd_last:
+                units.append((j - FILL_BEHIND, 2))
 
         for step in range(len(units) + SCALAR_LAG + 1):
             if step < len(units):
                 j, s = units[step]
-                regroup(step, j, s, on_vector(s))
+                regroup(j, s, on_vector(j, s))
                 if s == SLICES - 1 and j + RAW_SLOTS < BLOCKS:
                     load_weights(j + RAW_SLOTS)
             for lag, vector in ((SCALAR_LAG, False), (VECTOR_LAG, True)):
-                if 0 <= step - lag < len(units) and on_vector(units[step - lag][1]) == vector:
+                if 0 <= step - lag < len(units) and on_vector(units[step - lag][0], units[step - lag][1]) == vector:
                     quantise(units[step - lag][0], units[step - lag][1])
             block, place = divmod(step, SLICES)
             quarter = block - X_BEHIND
@@ -280,62 +314,38 @@ def tile_switchnet_fstar_pa_kernel(tc, x, k1, b1, out):
                 copy_x(quarter - 1)
             if place == 1 and 2 <= quarter <= X_QUARTERS + 1:
                 quantise_x(quarter - 2)
-            if step < len(units) and units[step][0] >= FIRST_LATE and units[step][1] == 1:
-                i = units[step][0] - FIRST_LATE
-                if i == 0:
-                    for h in range(SLICE_PIECES):
-                        multiply(h, 0, EARLY_BANKS)
-                        new_piece(h)
-                if i < EARLY_BANKS:
-                    for h in range(SLICE_PIECES):
-                        add_bias(h, i, i + 1)
             if place == 3 and block >= 1 and copied[0] < EARLY_BIAS_GROUPS:
                 if spread[0] < EARLY_BIAS_GROUPS:
                     next_spread()
                 next_copy()
+            if step < len(units) and units[step][0] in ROUND_BLOCKS and units[step][1] < 2:
+                q = ROUND_BLOCKS.index(units[step][0])
+                if units[step][1] == 0:
+                    multiply_banks(banks_of(0, PIECE_SLOTS, q, q + 1))
+                else:
+                    add_round(banks_of(0, PIECE_SLOTS, q, q + 1), [(FIRST_LATE + q, 2)])
 
-        late_step = {}
-
-        def late_units(first, last):
-            for i in range(first, last):
-                late_step[i] = len(units) + i
-                regroup(late_step[i], late[i][0], late[i][1], False)
-
-        def late_units_on_gpsimd(first, last, newest_read):
-            for n, i in enumerate(range(first, last)):
-                late_step[i] = late_step[newest_read - n]
-                j, s = late[i]
-                grouped[(j, s)] = stage.tile([P, PACK * UNIT_COLS], BF16, name="unit%d_%d" % (j, s),
-                                             offset=UNIT_BASE + (late_step[i] % UNIT_SLOTS) * UNIT_BYTES,
-                                             align_bytes=64)
-                by_piece = grouped[(j, s)][:].rearrange("p (h m r t) -> p h m r t", h=SLICE_PIECES, m=M_BLOCKS, t=PACK)
-                raw_by_piece = raw[j][:].rearrange("p t (m s h r) -> p s h m r t", m=M_BLOCKS, s=SLICES, h=SLICE_PIECES)
-                for h in range(SLICE_PIECES):
-                    nc.gpsimd.tensor_scalar(out=by_piece[:, h], in0=raw_by_piece[:, s, h],
-                                            scalar1=1.0, scalar2=0.0, op0=MULT, op1=ADD)
-
-        def late_quantise(first, last):
-            for i in range(first, last):
-                quantise(late[i][0], late[i][1])
-
-        def late_bias():
-            for group in range(SLICE_GROUPS):
-                next_spread()
-                next_copy()
-
-        for h in range(SLICE_PIECES):
-            multiply(h, EARLY_BANKS, PIECE_BANKS)
-        for h in range(SLICE_PIECES):
-            add_bias(h, EARLY_BANKS, PIECE_BANKS)
-            store(h)
-        late_units(0, len(late) // 2)
-        late_bias()
-        late_quantise(0, LATE_AFTER_SLICE_0)
-        late_units_on_gpsimd(len(late) // 2, LATE_AFTER_SLICE_1, LATE_AFTER_SLICE_0 - 1)
-        finish_slice(1)
-        late_bias()
-        late_quantise(LATE_AFTER_SLICE_0, LATE_AFTER_SLICE_1)
-        late_units_on_gpsimd(LATE_AFTER_SLICE_1, len(late), LATE_AFTER_SLICE_1 - 1)
-        finish_slice(2)
-        late_quantise(LATE_AFTER_SLICE_1, len(late))
-        finish_slice(3)
+        early_banks = len(ROUND_BLOCKS)
+        last_bank = PIECE_BANKS - 1
+        scalar_late = [(j, 3) for j in range(FIRST_LATE, first_gpsimd_last)]
+        multiply_banks(banks_of(0, 2, early_banks, PIECE_BANKS))
+        for j, s in scalar_late[:2]:
+            regroup(j, s, False)
+        add_round(banks_of(0, PIECE_SLOTS, early_banks, PIECE_BANKS),
+                  [(j, 2) for j in range(first_gpsimd_last, BLOCKS)],
+                  banks_of(2, PIECE_SLOTS, early_banks, PIECE_BANKS))
+        bias_groups(SLICE_GROUPS)
+        for j, s in scalar_late[2:4]:
+            regroup(j, s, False)
+        multiply_banks(banks_of(4, 6, 0, last_bank))
+        add_round(banks_of(4, 6, 0, PIECE_BANKS),
+                  [(j, 3) for j in range(first_gpsimd_last, BLOCKS)],
+                  banks_of(4, 6, last_bank, PIECE_BANKS))
+        bias_groups(SLICE_GROUPS)
+        for j, s in scalar_late[4:]:
+            regroup(j, s, False)
+        for j, s in scalar_late:
+            quantise(j, s)
+        multiply_banks(banks_of(6, 8, 0, last_bank))
+        add_round(banks_of(6, 7, 0, PIECE_BANKS), [], banks_of(6, 8, last_bank, PIECE_BANKS), 2)
+        add_round(banks_of(7, 8, 0, PIECE_BANKS), [], (), 2)

@@ -51,6 +51,7 @@ FIRST_LATE = 8
 GPSIMD_FIRST = 2
 GPSIMD_LAST = 3
 FILL_BEHIND = 3
+PUT_OFF = 2
 ROUND_BLOCKS = (9, 12)
 VECTOR_LAG = 1
 SCALAR_LAG = 4
@@ -66,6 +67,11 @@ X_SORTED_BASE = WIDE_BASE + X_QUARTERS * QUARTER_BYTES
 X_GROUPED_BASE = X_SORTED_BASE + 2 * QUARTER_BYTES
 PIECE_BYTES = PIECE_R * JM * 4
 PIECE_SLOTS = 4
+PIECE_BASE = (
+    [WIDE_BASE + h * PIECE_BYTES for h in range(4)]
+    + [((FIRST_LATE - 2 + h) % RAW_SLOTS) * RAW_BYTES for h in range(2)]
+    + [WIDE_BASE + h * PIECE_BYTES for h in range(2)]
+)
 
 FLOPS = 2 * P * K_BLOCK * COLS * BLOCKS
 
@@ -202,7 +208,7 @@ def tile_switchnet_fstar_pa_kernel(tc, x, k1, b1, out):
 
         def new_piece(h):
             pieces[h] = stage.tile([P, PIECE_R, JM], F32, name="piece%d" % h,
-                                   offset=WIDE_BASE + (h % PIECE_SLOTS) * PIECE_BYTES,
+                                   offset=PIECE_BASE[h],
                                    align_bytes=64)
 
         def add_bias(h, first_bank, last_bank, part=0, parts=1):
@@ -263,9 +269,12 @@ def tile_switchnet_fstar_pa_kernel(tc, x, k1, b1, out):
         riding = []
         added = {}
 
-        def add_round(tasks, ride, after_ride=(), parts=1):
-            for j, s in riding:
-                quantise(j, s)
+        def add_round(tasks, ride, after_ride=(), parts=1, quantise_first=True):
+            if quantise_first:
+                for j, s in riding:
+                    quantise(j, s)
+            else:
+                put_off.extend(riding)
             riding.clear()
             for j, s in ride:
                 regroup_on_gpsimd(j, s)
@@ -290,11 +299,14 @@ def tile_switchnet_fstar_pa_kernel(tc, x, k1, b1, out):
 
         first_gpsimd_last = BLOCKS - GPSIMD_LAST
         units = []
+        put_off = []
         for j in range(BLOCKS):
             for s in range(SLICES if j < FIRST_LATE else 2):
                 units.append((j, s))
             if FIRST_LATE + GPSIMD_FIRST <= j - FILL_BEHIND < first_gpsimd_last:
                 units.append((j - FILL_BEHIND, 2))
+                if j >= BLOCKS - PUT_OFF:
+                    put_off.append((j - FILL_BEHIND, 2))
 
         for step in range(len(units) + SCALAR_LAG + 1):
             if step < len(units):
@@ -304,7 +316,8 @@ def tile_switchnet_fstar_pa_kernel(tc, x, k1, b1, out):
                     load_weights(j + RAW_SLOTS)
             for lag, vector in ((SCALAR_LAG, False), (VECTOR_LAG, True)):
                 if 0 <= step - lag < len(units) and on_vector(units[step - lag][0], units[step - lag][1]) == vector:
-                    quantise(units[step - lag][0], units[step - lag][1])
+                    if units[step - lag] not in put_off:
+                        quantise(units[step - lag][0], units[step - lag][1])
             block, place = divmod(step, SLICES)
             quarter = block - X_BEHIND
             if place == 3 and 0 <= quarter < X_QUARTERS:
@@ -333,7 +346,9 @@ def tile_switchnet_fstar_pa_kernel(tc, x, k1, b1, out):
             regroup(j, s, False)
         add_round(banks_of(0, PIECE_SLOTS, early_banks, PIECE_BANKS),
                   [(j, 2) for j in range(first_gpsimd_last, BLOCKS)],
-                  banks_of(2, PIECE_SLOTS, early_banks, PIECE_BANKS))
+                  banks_of(2, PIECE_SLOTS, early_banks, PIECE_BANKS), 1, False)
+        for j, s in put_off:
+            quantise(j, s)
         bias_groups(SLICE_GROUPS)
         for j, s in scalar_late[2:4]:
             regroup(j, s, False)

@@ -23,7 +23,7 @@ PSUM_BANKS = 8
 SLICE_R = 32
 SLICES = R // SLICE_R
 UNIT_COLS = M_BLOCKS * SLICE_R
-RUN = 4
+RUN = 8
 PIECE_R = 16
 PIECES = R // PIECE_R
 SLICE_PIECES = PIECES // SLICES

from contextlib import ExitStack

import concourse.mybir as mybir
from concourse.masks import make_identity

BF16 = mybir.dt.bfloat16
F32 = mybir.dt.float32
U32 = mybir.dt.uint32
U8 = mybir.dt.uint8
FP8X4 = mybir.dt.float8_e4m3fn_x4
ADD = mybir.AluOpType.add
MULT = mybir.AluOpType.mult

P = 128
PACK = 4
BLOCKS = 16
K_BLOCK = P * PACK
COLS = 1024
M_BLOCKS = 8
R = 128
BANK_F32 = 512
PSUM_BANKS = 8
SLICE_R = 32
SLICES = R // SLICE_R
UNIT_COLS = M_BLOCKS * SLICE_R
RUN = 8
PIECE_R = 16
PIECES = R // PIECE_R
SLICE_PIECES = PIECES // SLICES
PASS_COLS = M_BLOCKS * PIECE_R
JM = BLOCKS * M_BLOCKS
BANK_BLOCKS = BANK_F32 // PASS_COLS
BANK_JM = BANK_BLOCKS * M_BLOCKS
PIECE_BANKS = BLOCKS // BANK_BLOCKS

X_QUARTERS = 4
QUARTER_BLOCKS = BLOCKS // X_QUARTERS
WINDOW_ROWS = 16
QUARTER_VALUES = QUARTER_BLOCKS * K_BLOCK
BLOCK_WORDS = K_BLOCK // 2
X_BEHIND = 2

GROUP_WORDS = BANK_F32 // JM
BIAS_GROUPS = R // (2 * GROUP_WORDS)
SLICE_GROUPS = BIAS_GROUPS // SLICES
EARLY_BIAS_GROUPS = 2 * SLICE_GROUPS
FIRST_SPREAD = 4
FIRST_COPIED = 2

FIRST_LATE = 8
GPSIMD_FIRST = 2
GPSIMD_LAST = 3
FILL_BEHIND = 3
PUT_OFF = 2
ROUND_BLOCKS = (9, 12)
VECTOR_LAG = 1
SCALAR_LAG = 4

RAW_SLOTS = 10
RAW_BYTES = PACK * COLS * 2
UNIT_SLOTS = 8
UNIT_BYTES = PACK * UNIT_COLS * 2
UNIT_BASE = RAW_SLOTS * RAW_BYTES
WIDE_BASE = UNIT_BASE + UNIT_SLOTS * UNIT_BYTES
QUARTER_BYTES = QUARTER_VALUES * 2
X_SORTED_BASE = WIDE_BASE + X_QUARTERS * QUARTER_BYTES
X_GROUPED_BASE = X_SORTED_BASE + 2 * QUARTER_BYTES
PIECE_BYTES = PIECE_R * JM * 4
PIECE_SLOTS = 4
PIECE_BASE = (
    [WIDE_BASE + h * PIECE_BYTES for h in range(4)]
    + [((FIRST_LATE - 2 + h) % RAW_SLOTS) * RAW_BYTES for h in range(2)]
    + [WIDE_BASE + h * PIECE_BYTES for h in range(2)]
)

FLOPS = 2 * P * K_BLOCK * COLS * BLOCKS


def on_vector(j, s):
    return s % 2 == 0 and (j < FIRST_LATE or s < 2)


def tile_switchnet_fstar_pa_kernel(tc, x, k1, b1, out):
    nc = tc.nc
    with ExitStack() as ctx:
        keep = ctx.enter_context(tc.tile_pool(name="keep", bufs=1))
        stage = ctx.enter_context(tc.tile_pool(name="stage", bufs=1))
        psum = ctx.enter_context(tc.psum_pool(name="psum", bufs=PSUM_BANKS))
        ctx.enter_context(tc.manual_schedule())

        identity = keep.tile([P, P], F32)
        bias_rows = keep.tile([P, R], BF16)
        bias = keep.tile([P, R * JM // 2], BF16)
        k_codes = keep.tile([P, BLOCKS, COLS], U32, align_bytes=64)
        k_scales = keep.tile([P, BLOCKS, COLS], U8, align_bytes=64)
        x_codes = keep.tile([P, BLOCKS * P], U32, align_bytes=64)
        x_scales = keep.tile([P, BLOCKS * P], U8, align_bytes=64)

        bias_row_words = bias_rows[:].bitcast(F32)
        bias_words = bias[:].bitcast(F32)
        bias_by_r = bias[:].rearrange("p (w g e) -> p w e g", g=JM, e=2)
        x_quarters = x.rearrange("b (a g) c -> b a (g c)", a=X_QUARTERS)

        raw = {}
        grouped = {}
        slot_of = {}
        x_loaded = {}
        x_sorted = {}
        x_grouped = {}
        banks = {}
        pieces = {}

        def bank(key, shape):
            banks[key] = psum.tile(shape, F32, name="bank", tag="bank")
            return banks[key]

        def load_weights(j):
            raw[j] = stage.tile([P, PACK, COLS], BF16, name="raw%d" % j,
                                offset=(j % RAW_SLOTS) * RAW_BYTES, align_bytes=64)
            nc.sync.dma_start(out=raw[j][:], in_=k1[j].rearrange("(p t) l -> p t l", t=PACK))

        def load_x(quarter):
            x_loaded[quarter] = stage.tile([P, QUARTER_VALUES], BF16, name="x_loaded%d" % quarter,
                                           offset=WIDE_BASE + quarter * QUARTER_BYTES, align_bytes=64)
            nc.sync.dma_start(out=x_loaded[quarter][:], in_=x_quarters[:, quarter, :])

        def spread_bias(group):
            fanned = bank(("bias", group), [P, GROUP_WORDS, JM])
            for c in range(GROUP_WORDS):
                w = GROUP_WORDS * group + c
                nc.tensor.transpose(fanned[:, c, :], bias_row_words[:, w:w + 1].to_broadcast([P, P]), identity[:])

        def copy_bias(group):
            place = group % EARLY_BIAS_GROUPS
            nc.scalar.copy(out=bias_words[:, place * BANK_F32:(place + 1) * BANK_F32],
                           in_=banks[("bias", group)][:].rearrange("p c g -> p (c g)"))

        def sort_x(quarter):
            x_sorted[quarter] = stage.tile([P, QUARTER_VALUES], BF16, name="x_sorted%d" % quarter,
                                           offset=X_SORTED_BASE + (quarter % 2) * QUARTER_BYTES, align_bytes=64)
            nc.vector.tensor_copy(
                out=x_sorted[quarter][:].rearrange("p (c i v) -> p c i v", c=QUARTER_BLOCKS, i=WINDOW_ROWS),
                in_=x_loaded[quarter][:].rearrange("p (i c v) -> p c i v", c=QUARTER_BLOCKS, i=WINDOW_ROWS),
            )
            x_grouped[quarter] = stage.tile([P, QUARTER_VALUES], BF16, name="x_grouped%d" % quarter,
                                            offset=X_GROUPED_BASE + (quarter % 2) * QUARTER_BYTES, align_bytes=64)

        def transpose_x(quarter):
            words = x_sorted[quarter][:].bitcast(F32)
            for pair in range(QUARTER_BLOCKS // 2):
                turned = bank(("x", quarter, pair), [P, 2, 2, P])
                for c in range(2):
                    first = (2 * pair + c) * BLOCK_WORDS
                    for u in range(2):
                        nc.tensor.transpose(turned[:, c, u, :],
                                            words[:, first + u:first + BLOCK_WORDS:2], identity[:])

        def copy_x(quarter):
            words = x_grouped[quarter][:].bitcast(F32).rearrange("p (c b u) -> p c b u", c=QUARTER_BLOCKS, u=2)
            for pair in range(QUARTER_BLOCKS // 2):
                nc.scalar.copy(out=words[:, 2 * pair:2 * pair + 2],
                               in_=banks[("x", quarter, pair)][:].rearrange("p c u b -> p c b u"))

        def quantise_x(quarter):
            cols = slice(quarter * QUARTER_BLOCKS * P, (quarter + 1) * QUARTER_BLOCKS * P)
            nc.vector.quantize_mx(out=x_codes[:, cols].bitcast(FP8X4), scales=x_scales[:, cols],
                                  in_=x_grouped[quarter][:])

        free_slots = list(range(UNIT_SLOTS))

        def new_unit(j, s, slot):
            free_slots.remove(slot)
            slot_of[(j, s)] = slot
            grouped[(j, s)] = stage.tile([P, PACK * UNIT_COLS], BF16, name="unit%d_%d" % (j, s),
                                         offset=UNIT_BASE + slot * UNIT_BYTES, align_bytes=64)

        def regroup(j, s, vector):
            new_unit(j, s, free_slots[0])
            by_piece = grouped[(j, s)][:].rearrange("p (h m c i t) -> p h m c t i", h=SLICE_PIECES, m=M_BLOCKS, i=RUN, t=PACK)
            raw_by_piece = raw[j][:].rearrange("p t (m s h c i) -> p s h m c t i", m=M_BLOCKS, s=SLICES, h=SLICE_PIECES, i=RUN)
            for h in range(SLICE_PIECES):
                if vector:
                    nc.vector.tensor_copy(out=by_piece[:, h], in_=raw_by_piece[:, s, h])
                else:
                    nc.scalar.copy(out=by_piece[:, h], in_=raw_by_piece[:, s, h])

        def quantise(j, s):
            cols = slice(s * UNIT_COLS, (s + 1) * UNIT_COLS)
            nc.vector.quantize_mx(out=k_codes[:, j, cols].bitcast(FP8X4), scales=k_scales[:, j, cols],
                                  in_=grouped[(j, s)][:])
            free_slots.append(slot_of[(j, s)])

        def multiply(h, first_bank=0, last_bank=PIECE_BANKS):
            cols = slice(h * PASS_COLS, (h + 1) * PASS_COLS)
            for q in range(first_bank, last_bank):
                acc = bank(("y", h, q), [P, BANK_F32])
                for c in range(BANK_BLOCKS):
                    j = BANK_BLOCKS * q + c
                    nc.tensor.matmul_mx(
                        out=acc[:, c * PASS_COLS:(c + 1) * PASS_COLS],
                        lhsT=x_codes[:, j * P:(j + 1) * P].bitcast(FP8X4),
                        lhsT_scale=x_scales[:, j * P:(j + 1) * P],
                        rhs=k_codes[:, j, cols].bitcast(FP8X4),
                        rhs_scale=k_scales[:, j, cols],
                        start=True,
                        stop=True,
                    )

        def new_piece(h):
            pieces[h] = stage.tile([P, PIECE_R, JM], F32, name="piece%d" % h,
                                   offset=PIECE_BASE[h],
                                   align_bytes=64)

        def add_bias(h, first_bank, last_bank, part=0, parts=1):
            by_r = pieces[h][:].rearrange("p (w e) g -> p w e g", e=2)
            pairs = PIECE_R // 2 // parts
            in_piece = slice(part * pairs, (part + 1) * pairs)
            first_pair = (h % PIECE_SLOTS) * PIECE_R // 2
            in_bias = slice(first_pair + part * pairs, first_pair + (part + 1) * pairs)
            for q in range(first_bank, last_bank):
                jm = slice(q * BANK_JM, (q + 1) * BANK_JM)
                nc.vector.tensor_tensor(
                    out=by_r[:, in_piece, :, jm],
                    in0=banks[("y", h, q)][:].rearrange("p (g w e) -> p w e g", g=BANK_JM, e=2)[:, in_piece],
                    in1=bias_by_r[:, in_bias, :, jm],
                    op=ADD,
                )

        def store(h, part=0, parts=1):
            rows = PIECE_R // parts
            nc.sync.dma_start(out=out[:, h * PIECE_R + part * rows:h * PIECE_R + (part + 1) * rows, :],
                              in_=pieces[h][:, part * rows:(part + 1) * rows, :])

        nc.sync.dma_start(out=bias_rows[:], in_=b1.rearrange("o j (m r) -> (o j m) r", r=R))
        make_identity(nc, identity[:])
        for j in range(RAW_SLOTS):
            load_weights(j)
            if 0 <= j - X_BEHIND < X_QUARTERS:
                load_x(j - X_BEHIND)

        spread = [0]
        copied = [0]

        def next_spread():
            spread_bias(spread[0])
            spread[0] += 1

        def next_copy():
            copy_bias(copied[0])
            copied[0] += 1

        for group in range(FIRST_SPREAD):
            next_spread()
        for group in range(FIRST_COPIED):
            next_copy()

        def regroup_on_gpsimd(j, s):
            new_unit(j, s, free_slots[-1])
            by_piece = grouped[(j, s)][:].rearrange("p (h m r t) -> p h m r t", h=SLICE_PIECES, m=M_BLOCKS, t=PACK)
            raw_by_piece = raw[j][:].rearrange("p t (m s h r) -> p s h m r t", m=M_BLOCKS, s=SLICES, h=SLICE_PIECES)
            for h in range(SLICE_PIECES):
                nc.gpsimd.tensor_scalar(out=by_piece[:, h], in0=raw_by_piece[:, s, h],
                                        scalar1=1.0, scalar2=0.0, op0=MULT, op1=ADD)

        def multiply_banks(tasks):
            for h, q in tasks:
                multiply(h, q, q + 1)

        riding = []
        added = {}

        def add_round(tasks, ride, after_ride=(), parts=1, quantise_first=True):
            if quantise_first:
                for j, s in riding:
                    quantise(j, s)
            else:
                put_off.extend(riding)
            riding.clear()
            for j, s in ride:
                regroup_on_gpsimd(j, s)
                riding.append((j, s))
            multiply_banks(after_ride)
            for part in range(parts):
                for h, q in tasks:
                    if h not in pieces:
                        new_piece(h)
                    add_bias(h, q, q + 1, part, parts)
                    added[h] = added.get(h, 0) + 1
                    if added[h] % PIECE_BANKS == 0:
                        store(h, part, parts)

        def bias_groups(count):
            for group in range(count):
                next_spread()
                next_copy()

        def banks_of(first_piece, last_piece, first_bank, last_bank):
            return [(h, q) for h in range(first_piece, last_piece) for q in range(first_bank, last_bank)]

        first_gpsimd_last = BLOCKS - GPSIMD_LAST
        units = []
        put_off = []
        for j in range(BLOCKS):
            for s in range(SLICES if j < FIRST_LATE else 2):
                units.append((j, s))
            if FIRST_LATE + GPSIMD_FIRST <= j - FILL_BEHIND < first_gpsimd_last:
                units.append((j - FILL_BEHIND, 2))
                if j >= BLOCKS - PUT_OFF:
                    put_off.append((j - FILL_BEHIND, 2))

        for step in range(len(units) + SCALAR_LAG + 1):
            if step < len(units):
                j, s = units[step]
                regroup(j, s, on_vector(j, s))
                if s == SLICES - 1 and j + RAW_SLOTS < BLOCKS:
                    load_weights(j + RAW_SLOTS)
            for lag, vector in ((SCALAR_LAG, False), (VECTOR_LAG, True)):
                if 0 <= step - lag < len(units) and on_vector(units[step - lag][0], units[step - lag][1]) == vector:
                    if units[step - lag] not in put_off:
                        quantise(units[step - lag][0], units[step - lag][1])
            block, place = divmod(step, SLICES)
            quarter = block - X_BEHIND
            if place == 3 and 0 <= quarter < X_QUARTERS:
                sort_x(quarter)
                transpose_x(quarter)
            if place == 1 and 1 <= quarter <= X_QUARTERS:
                copy_x(quarter - 1)
            if place == 1 and 2 <= quarter <= X_QUARTERS + 1:
                quantise_x(quarter - 2)
            if place == 3 and block >= 1 and copied[0] < EARLY_BIAS_GROUPS:
                if spread[0] < EARLY_BIAS_GROUPS:
                    next_spread()
                next_copy()
            if step < len(units) and units[step][0] in ROUND_BLOCKS and units[step][1] < 2:
                q = ROUND_BLOCKS.index(units[step][0])
                if units[step][1] == 0:
                    multiply_banks(banks_of(0, PIECE_SLOTS, q, q + 1))
                else:
                    add_round(banks_of(0, PIECE_SLOTS, q, q + 1), [(FIRST_LATE + q, 2)])

        early_banks = len(ROUND_BLOCKS)
        last_bank = PIECE_BANKS - 1
        scalar_late = [(j, 3) for j in range(FIRST_LATE, first_gpsimd_last)]
        multiply_banks(banks_of(0, 2, early_banks, PIECE_BANKS))
        for j, s in scalar_late[:2]:
            regroup(j, s, False)
        add_round(banks_of(0, PIECE_SLOTS, early_banks, PIECE_BANKS),
                  [(j, 2) for j in range(first_gpsimd_last, BLOCKS)],
                  banks_of(2, PIECE_SLOTS, early_banks, PIECE_BANKS), 1, False)
        for j, s in put_off:
            quantise(j, s)
        bias_groups(SLICE_GROUPS)
        for j, s in scalar_late[2:4]:
            regroup(j, s, False)
        multiply_banks(banks_of(4, 6, 0, last_bank))
        add_round(banks_of(4, 6, 0, PIECE_BANKS),
                  [(j, 3) for j in range(first_gpsimd_last, BLOCKS)],
                  banks_of(4, 6, last_bank, PIECE_BANKS))
        bias_groups(SLICE_GROUPS)
        for j, s in scalar_late[4:]:
            regroup(j, s, False)
        for j, s in scalar_late:
            quantise(j, s)
        multiply_banks(banks_of(6, 8, 0, last_bank))
        add_round(banks_of(6, 7, 0, PIECE_BANKS), [], banks_of(6, 8, last_bank, PIECE_BANKS), 2)
        add_round(banks_of(7, 8, 0, PIECE_BANKS), [], (), 2)
